import numpy as np
import ml_dtypes


def mxq(x, axis, fmt="e4m3"):
    dtype, down = {"e4m3": (ml_dtypes.float8_e4m3fn, 7), "e5m2": (ml_dtypes.float8_e5m2, 14)}[fmt]
    v = np.moveaxis(np.asarray(x, np.float32).astype(ml_dtypes.bfloat16).astype(np.float64), axis, -1)
    blocks = v.reshape(v.shape[:-1] + (-1, 32))
    amax = np.abs(blocks).max(-1, keepdims=True)
    byte = np.maximum(np.where(amax > 0, np.frexp(amax)[1] - 1 + 127, 0) - down, 1)
    scale = np.exp2(byte - 127.0)
    codes = (blocks / scale).astype(np.float32).astype(dtype).astype(np.float64)
    return np.moveaxis((codes * scale).reshape(v.shape), -1, axis)


WIDE = False


def mx_kscale(k):
    if not WIDE:
        return np.ones(k)
    levels = np.array([10, -10, 5, -5, 0])
    a = np.random.permutation(np.resize(levels, k // 512 * 4)).reshape(k // 512, 4)
    idx = np.arange(k)
    return np.exp2(a[idx // 512, idx % 128 // 32])


BF16 = ml_dtypes.bfloat16


def bf(x):
    return np.asarray(x, np.float32).astype(BF16)


def f64(x):
    return np.asarray(x).astype(np.float64)


B, S, IN, OUT, GROUP = 4, 1024, 1024, 1024, 128
SCALE_RATIO = 1.4171
EPS = 1e-6


def softplus(v):
    return np.logaddexp(v, 0.0)


def inv_softplus(b):
    return np.where(b > 30.0, b, np.log(np.expm1(np.minimum(b, 30.0)) + EPS))


def setup_inputs():
    s = mx_kscale(IN)
    hi, lo = s.max(), s.min()
    sg = np.resize(np.array([hi, lo, np.sqrt(hi), np.sqrt(lo)]) / hi, IN // GROUP)
    x = np.random.standard_normal((B, S, IN)) * np.repeat(sg, GROUP)
    latent = np.random.standard_normal((OUT, IN)) / np.sqrt(IN)
    base_scale = np.abs(latent.reshape(OUT, IN // GROUP, GROUP)).mean(axis=-1) * SCALE_RATIO
    base_scale = base_scale * np.exp2(np.random.uniform(-1.0, 1.0, (OUT, IN // GROUP)))
    raw_scales = inv_softplus(base_scale / sg)
    return {"x": bf(x), "weight_logits": bf(latent), "raw_scales": bf(raw_scales)}


def reference(x, weight_logits, raw_scales):
    wl = f64(weight_logits)
    rows, cols = wl.shape
    g = wl.reshape(rows, cols // GROUP, GROUP)
    q = np.where(g >= 0, 1.0, -1.0)
    signed = g + (q - g)
    scales = softplus(f64(raw_scales)) + EPS
    w = (signed * scales[:, :, None]).reshape(rows, cols)
    return mxq(f64(x), 2, "e4m3") @ mxq(w, 1, "e4m3").T

@@ -1,0 +1,313 @@
+from contextlib import ExitStack
+
+import concourse.mybir as mybir
+from concourse.masks import make_identity
+
+FLOPS = 2 * 4096 * 1024 * 1024
+
+BF16 = mybir.dt.bfloat16
+F32 = mybir.dt.float32
+U32 = mybir.dt.uint32
+U8 = mybir.dt.uint8
+FP8X4 = mybir.dt.float8_e4m3fn_x4
+ALU = mybir.AluOpType
+ACT = mybir.ActivationFunctionType
+
+I32 = mybir.dt.int32
+
+LOG2E = 1.4426950408889634
+LN2HI = 0.693359375
+LN2LO = 0.6931471805599453 - 0.693359375
+AT_ALPHA = -4.440468600468879
+AT_BETA = -31.55953139953112
+AT_GAMMA = 176.6608917748704
+AT_B1 = 4.0 * -45738.0 / 8721.0
+AT_B0 = 16.0 * 45045.0 / 8721.0
+AT_KAPPA = 8721.0 / -11025.0
+
+P = 128
+K = 1024
+O = 1024
+NT = 32
+CH = 4
+NCH = NT // CH
+NOT = O // P
+
+
+def tile_groupedstelinear_t_kernel(tc, x, weight_logits, raw_scales, out):
+    nc = tc.nc
+    xv = x.flatten_outer_dims().rearrange("(p t) k -> p t k", t=NT)
+    ov = out.flatten_outer_dims().rearrange("(p t) o -> p t o", t=NT)
+    wv = weight_logits.rearrange("(t p) i -> p t i", p=P)
+    sv = raw_scales.rearrange("(t p) g -> p t g", p=P)
+
+    with ExitStack() as ctx:
+        const = ctx.enter_context(tc.tile_pool(name="const", bufs=1))
+        hsp = ctx.enter_context(tc.tile_pool(name="hsp", bufs=4))
+        wsp = ctx.enter_context(tc.tile_pool(name="wsp", bufs=3))
+        xsp = ctx.enter_context(tc.tile_pool(name="xsp", bufs=2))
+        xgp = ctx.enter_context(tc.tile_pool(name="xgp", bufs=2))
+        xcp = ctx.enter_context(tc.tile_pool(name="xcp", bufs=3))
+        osp = ctx.enter_context(tc.tile_pool(name="osp", bufs=6))
+        psum = ctx.enter_context(tc.psum_pool(name="psum", bufs=8))
+        ctx.enter_context(tc.manual_schedule())
+
+        sraw = const.tile([P, NOT, 8], BF16, name="sraw")
+        nc.sync.dma_start(out=sraw[:], in_=sv)
+        wraw = [const.tile([P, 2, K], BF16, name="wraw%d" % j) for j in range(4)]
+        xraw = [const.tile([P, CH, K], BF16, name="xraw%d" % c) for c in range(NCH)]
+
+        def load_w(j):
+            nc.sync.dma_start(out=wraw[j][:], in_=wv[:, 2 * j : 2 * j + 2, :])
+
+        def load_x(c):
+            nc.sync.dma_start(out=xraw[c][:], in_=xv[:, CH * c : CH * c + CH, :])
+
+        load_x(0)
+        load_w(0)
+        load_w(1)
+        load_x(1)
+        load_w(2)
+        load_w(3)
+        for c in range(2, NCH):
+            load_x(c)
+
+        ident_b = const.tile([P, P], BF16, name="ident_b")
+        make_identity(nc, ident_b[:])
+        ident_f = const.tile([P, P], F32, name="ident_f")
+        make_identity(nc, ident_f[:])
+
+        hs = {}
+
+        def half_sign(t):
+            hs[t] = hsp.tile([P, K], BF16, name="hs", tag="hs")
+            nc.vector.tensor_scalar(
+                out=hs[t][:], in0=wraw[t // 2][:, t % 2, :], scalar1=0.0, scalar2=0.5,
+                op0=ALU.is_ge, op1=ALU.subtract,
+            )
+
+        v = sraw[:].rearrange("p t g -> p (t g)")
+
+        def f32tile(name):
+            return const.tile([P, 64], F32, name=name)
+
+        def stt(name, in0, scalar, op0, in1, op1):
+            o = f32tile(name)
+            nc.vector.scalar_tensor_tensor(
+                out=o[:], in0=in0, scalar=scalar, in1=in1, op0=op0, op1=op1
+            )
+            return o[:]
+
+        def ts(name, in0, s1, op0, s2_=None, op1=None, dt=F32):
+            o = const.tile([P, 64], dt, name=name)
+            if op1 is None:
+                nc.vector.tensor_scalar(out=o[:], in0=in0, scalar1=s1, scalar2=None, op0=op0)
+            else:
+                nc.vector.tensor_scalar(
+                    out=o[:], in0=in0, scalar1=s1, scalar2=s2_, op0=op0, op1=op1
+                )
+            return o[:]
+
+        def tt(name, in0, in1, op):
+            o = f32tile(name)
+            nc.vector.tensor_tensor(out=o[:], in0=in0, in1=in1, op=op)
+            return o[:]
+
+        def rcp(name, in_):
+            o = f32tile(name)
+            nc.vector.reciprocal(out=o[:], in_=in_)
+            return o[:]
+
+        na = stt("na", v, -1.0, ALU.mult, v, ALU.min)
+        ni = ts("ni", na, LOG2E, ALU.mult, -126.0, ALU.max, dt=I32)
+        rh = stt("rh", ni, -LN2HI, ALU.mult, na, ALU.add)
+        lo = ts("lo", ni, -LN2LO, ALU.mult)
+        pw = ts("pw", ni, 127.0, ALU.add, 8388608.0, ALU.mult, dt=I32)
+        p2 = pw.bitcast(F32)
+        r = stt("r", rh, -1.0, ALU.max, lo, ALU.add)
+        t1 = ts("t1", p2, 2.0, ALU.add)
+        t2 = ts("t2", p2, 2.0, ALU.subtract)
+        w = tt("w", r, r, ALU.mult)
+        rt = tt("rt", r, t2, ALU.mult)
+        rp = tt("rp", r, p2, ALU.mult)
+        a1 = stt("a1", w, 180.0, ALU.add, w, ALU.mult)
+        bl = ts("bl", w, 20.0, ALU.mult, 840.0, ALU.add)
+        at = stt("at", a1, 1680.0, ALU.add, t1, ALU.mult)
+        bt = tt("bt", bl, rt, ALU.mult)
+        ap = stt("ap", a1, 1680.0, ALU.add, p2, ALU.mult)
+        bp = tt("bp", bl, rp, ALU.mult)
+        q = tt("q", at, bt, ALU.add)
+        pp = tt("pp", ap, bp, ALU.add)
+        rq = rcp("rq", q)
+        half_sign(0)
+        z = stt("z", pp, 2.0, ALU.mult, rq, ALU.mult)
+        half_sign(1)
+        zz = tt("zz", z, z, ALU.mult)
+        m = stt("m", v, 0.0, ALU.max, z, ALU.add)
+        f1 = ts("f1", zz, AT_ALPHA, ALU.add)
+        f2 = stt("f2", zz, AT_BETA, ALU.add, zz, ALU.mult)
+        g1 = stt("g1", zz, AT_B1, ALU.add, zz, ALU.mult)
+        zw = tt("zw", z, zz, ALU.mult)
+        dm = stt("dm", f2, AT_GAMMA, ALU.add, f1, ALU.mult)
+        g2 = stt("g2", g1, AT_B0, ALU.add, zw, ALU.mult)
+        ru = rcp("ru", dm)
+        half_sign(2)
+        corr = stt("corr", g2, AT_KAPPA, ALU.mult, ru, ALU.mult)
+        half_sign(3)
+        sc = stt("sc", corr, 1e-6, ALU.add, m, ALU.add)
+
+        wgrp = const.tile([P, 2, O * 4], BF16, name="wgrp", align_bytes=64)
+        wcod = const.tile([P, 2, O], U32, name="wcod", align_bytes=64)
+        wpla = const.tile([P, 2, O], U8, name="wpla", align_bytes=64)
+        wt = {}
+
+        def build_w(t):
+            ws = wsp.tile([P, K], BF16, name="ws", tag="ws")
+            for grp in range(8):
+                nc.vector.tensor_scalar(
+                    out=ws[:, grp * P : (grp + 1) * P],
+                    in0=hs[t][:, grp * P : (grp + 1) * P],
+                    scalar1=2.0,
+                    scalar2=sc[:, t * 8 + grp : t * 8 + grp + 1],
+                    op0=ALU.mult,
+                    op1=ALU.mult,
+                )
+            wt[t] = psum.tile([P, 8, P], BF16, name="wt", tag="bank")
+            for g in range(2):
+                for j in range(4):
+                    nc.tensor.transpose(
+                        wt[t][:, 4 * g + j, :],
+                        ws[:, 512 * g + j : 512 * g + 512 : 4],
+                        ident_b[:],
+                    )
+
+        def evac_w(t):
+            nc.scalar.copy(
+                out=wgrp[:].rearrange("p g (o t) -> p g o t", t=4)[:, :, t * P : (t + 1) * P, :],
+                in_=wt[t][:].rearrange("p (g t) o -> p g o t", g=2),
+            )
+
+        def quant_w(j):
+            for g in range(2):
+                nc.vector.quantize_mx(
+                    out=wcod[:, g, 256 * j : 256 * j + 256].bitcast(FP8X4),
+                    scales=wpla[:, g, 256 * j : 256 * j + 256],
+                    in_=wgrp[:, g, 1024 * j : 1024 * j + 1024],
+                )
+
+        xs = {}
+        xt = {}
+        xg = {}
+        xc = {}
+        xp = {}
+
+        def presort(c):
+            xs[c] = xsp.tile([P, CH, K], BF16, name="xs", tag="xs")
+            nc.vector.tensor_copy(
+                out=xs[c][:].rearrange("p i k -> p (i k)").bitcast(F32).rearrange(
+                    "p (m u q) -> p m u q", u=2, q=P
+                ),
+                in_=xraw[c][:].rearrange("p i k -> p (i k)").bitcast(F32).rearrange(
+                    "p (m q u) -> p m u q", u=2, q=P
+                ),
+            )
+
+        def transpose_x(c, direct=False):
+            for i in range(CH):
+                xt[c, i] = psum.tile([P, 4, P], F32, name="xt", tag="bank")
+                if direct:
+                    words = xraw[c][:, i, :].bitcast(F32)
+                    for j in range(4):
+                        g, u = divmod(j, 2)
+                        nc.tensor.transpose(
+                            xt[c, i][:, j, :],
+                            words[:, 256 * g + u : 256 * g + 256 : 2],
+                            ident_f[:],
+                        )
+                else:
+                    words = xs[c][:, i, :].bitcast(F32)
+                    for j in range(4):
+                        nc.tensor.transpose(
+                            xt[c, i][:, j, :], words[:, P * j : P * (j + 1)], ident_f[:]
+                        )
+
+        def evac_x(c, eng):
+            xg[c] = xgp.tile([P, CH, K], BF16, name="xg", tag="xg", align_bytes=64)
+            for i in range(CH):
+                dst = xg[c][:, i, :].bitcast(F32).rearrange("p (g o u) -> p g o u", g=2, u=2)
+                src = xt[c, i][:].rearrange("p (g u) o -> p g o u", u=2)
+                if eng == "s":
+                    nc.scalar.copy(out=dst, in_=src)
+                else:
+                    nc.vector.tensor_copy(out=dst, in_=src)
+
+        def quant_x(c):
+            xc[c] = xcp.tile([P, CH * 256], U32, name="xc", tag="xc", align_bytes=64)
+            xp[c] = xcp.tile([P, CH * 256], U8, name="xp", tag="xp", align_bytes=64)
+            nc.vector.quantize_mx(
+                out=xc[c][:].bitcast(FP8X4),
+                scales=xp[c][:],
+                in_=xg[c][:].rearrange("p i k -> p (i k)"),
+            )
+
+        def multiply(c):
+            ost = None
+            for i in range(CH):
+                if i % 2 == 0:
+                    ost = osp.tile([P, 2, O], F32, name="ost", tag="ost")
+                for h in range(2):
+                    acc = psum.tile([P, 512], F32, name="acc", tag="bank")
+                    for g in range(2):
+                        col = (2 * i + g) * P
+                        nc.tensor.matmul_mx(
+                            out=acc[:],
+                            lhsT=xc[c][:, col : col + P].bitcast(FP8X4),
+                            lhsT_scale=xp[c][:, col : col + P],
+                            rhs=wcod[:, g, 512 * h : 512 * h + 512].bitcast(FP8X4),
+                            rhs_scale=wpla[:, g, 512 * h : 512 * h + 512],
+                            start=(g == 0),
+                            stop=(g == 1),
+                        )
+                    nc.scalar.copy(out=ost[:, i % 2, 512 * h : 512 * h + 512], in_=acc[:])
+                t = CH * c + i
+                if c == NCH - 1 and i >= 2:
+                    nc.sync.dma_start(out=ov[:, t : t + 1, :], in_=ost[:, i % 2 : i % 2 + 1, :])
+                elif i % 2 == 1:
+                    nc.sync.dma_start(out=ov[:, t - 1 : t + 1, :], in_=ost[:])
+
+        transpose_x(0, direct=True)
+        evac_x(0, "s")
+        transpose_x(1, direct=True)
+        evac_x(1, "s")
+        for t in range(4):
+            build_w(t)
+            evac_w(t)
+        quant_x(0)
+        half_sign(4)
+        build_w(4)
+        evac_w(4)
+        half_sign(5)
+        build_w(5)
+        evac_w(5)
+        quant_w(0)
+        half_sign(6)
+        build_w(6)
+        evac_w(6)
+        half_sign(7)
+        build_w(7)
+        evac_w(7)
+        quant_w(1)
+        quant_x(1)
+        quant_w(2)
+        presort(2)
+        quant_w(3)
+
+        for r in range(NCH):
+            if r + 2 < NCH:
+                transpose_x(r + 2)
+                evac_x(r + 2, "v")
+            if r + 3 < NCH:
+                presort(r + 3)
+            if r + 2 < NCH:
+                quant_x(r + 2)
+            multiply(r)

@@ -7,13 +7,11 @@ FLOPS = 2 * 4096 * 1024 * 1024
 
 BF16 = mybir.dt.bfloat16
 F32 = mybir.dt.float32
+I32 = mybir.dt.int32
 U32 = mybir.dt.uint32
 U8 = mybir.dt.uint8
 FP8X4 = mybir.dt.float8_e4m3fn_x4
 ALU = mybir.AluOpType
-ACT = mybir.ActivationFunctionType
-
-I32 = mybir.dt.int32
 
 LOG2E = 1.4426950408889634
 LN2HI = 0.693359375
@@ -45,7 +43,7 @@ def tile_groupedstelinear_t_kernel(tc, x, weight_logits, raw_scales, out):
         const = ctx.enter_context(tc.tile_pool(name="const", bufs=1))
         hsp = ctx.enter_context(tc.tile_pool(name="hsp", bufs=4))
         wsp = ctx.enter_context(tc.tile_pool(name="wsp", bufs=3))
-        xsp = ctx.enter_context(tc.tile_pool(name="xsp", bufs=2))
+        xsp = ctx.enter_context(tc.tile_pool(name="xsp", bufs=8))
         xgp = ctx.enter_context(tc.tile_pool(name="xgp", bufs=2))
         xcp = ctx.enter_context(tc.tile_pool(name="xcp", bufs=3))
         osp = ctx.enter_context(tc.tile_pool(name="osp", bufs=6))
@@ -55,27 +53,81 @@ def tile_groupedstelinear_t_kernel(tc, x, weight_logits, raw_scales, out):
         sraw = const.tile([P, NOT, 8], BF16, name="sraw")
         nc.sync.dma_start(out=sraw[:], in_=sv)
         wraw = [const.tile([P, 2, K], BF16, name="wraw%d" % j) for j in range(4)]
-        xraw = [const.tile([P, CH, K], BF16, name="xraw%d" % c) for c in range(NCH)]
+        xraw = {}
+
+        def load_x(first, count):
+            t = const.tile([P, count, K], BF16, name="xraw%d" % first)
+            nc.sync.dma_start(out=t[:], in_=xv[:, first : first + count, :])
+            for i in range(count):
+                xraw[first + i] = t[:, i, :]
 
         def load_w(j):
             nc.sync.dma_start(out=wraw[j][:], in_=wv[:, 2 * j : 2 * j + 2, :])
 
-        def load_x(c):
-            nc.sync.dma_start(out=xraw[c][:], in_=xv[:, CH * c : CH * c + CH, :])
-
-        load_x(0)
-        load_w(0)
-        load_w(1)
-        load_x(1)
-        load_w(2)
-        load_w(3)
+        for i in range(4):
+            load_x(i, 1)
+        load_x(4, 2)
+        load_x(6, 2)
+        for j in range(4):
+            load_w(j)
         for c in range(2, NCH):
-            load_x(c)
+            load_x(CH * c, CH)
 
-        ident_b = const.tile([P, P], BF16, name="ident_b")
-        make_identity(nc, ident_b[:])
         ident_f = const.tile([P, P], F32, name="ident_f")
         make_identity(nc, ident_f[:])
+        ident_b = const.tile([P, P], BF16, name="ident_b")
+        make_identity(nc, ident_b[:])
+
+        xs = {}
+        xt = {}
+        xg = {}
+        xc = {}
+        xp = {}
+
+        def presort(t, eng):
+            xs[t] = xsp.tile([P, K], BF16, name="xs", tag="xs")
+            if eng == "s":
+                for g in range(2):
+                    nc.scalar.copy(
+                        out=xs[t][:, 512 * g : 512 * g + 512].bitcast(F32).rearrange(
+                            "p (u a r) -> p u a r", u=2, a=4
+                        ),
+                        in_=xraw[t][:, 512 * g : 512 * g + 512].bitcast(F32).rearrange(
+                            "p (a u r) -> p u a r", u=2, a=4
+                        ),
+                    )
+            else:
+                nc.vector.tensor_copy(
+                    out=xs[t][:].rearrange("p (g u a r) -> p g u a r", g=2, u=2, a=4),
+                    in_=xraw[t].rearrange("p (g a u r) -> p g u a r", g=2, u=2, a=4),
+                )
+
+        def transpose_x(t):
+            xt[t] = psum.tile([P, 4, P], F32, name="xt", tag="bank")
+            words = xs[t][:].bitcast(F32)
+            for j in range(4):
+                nc.tensor.transpose(xt[t][:, j, :], words[:, P * j : P * (j + 1)], ident_f[:])
+
+        def evac_x(t, eng):
+            c, i = divmod(t, CH)
+            if i == 0:
+                xg[c] = xgp.tile([P, CH, K], BF16, name="xg", tag="xg", align_bytes=64)
+            dst = xg[c][:, i, :].bitcast(F32).rearrange("p (g o u) -> p g o u", g=2, u=2)
+            src = xt[t][:].rearrange("p (g u) o -> p g o u", u=2)
+            if eng == "s":
+                nc.scalar.copy(out=dst, in_=src)
+            else:
+                nc.vector.tensor_copy(out=dst, in_=src)
+
+        def quant_x(c, first, count):
+            if first == 0:
+                xc[c] = xcp.tile([P, CH * 256], U32, name="xc", tag="xc", align_bytes=64)
+                xp[c] = xcp.tile([P, CH * 256], U8, name="xp", tag="xp", align_bytes=64)
+            nc.vector.quantize_mx(
+                out=xc[c][:, 256 * first : 256 * (first + count)].bitcast(FP8X4),
+                scales=xp[c][:, 256 * first : 256 * (first + count)],
+                in_=xg[c][:, first : first + count, :].rearrange("p i k -> p (i k)"),
+            )
 
         hs = {}
 
@@ -98,13 +150,13 @@ def tile_groupedstelinear_t_kernel(tc, x, weight_logits, raw_scales, out):
             )
             return o[:]
 
-        def ts(name, in0, s1, op0, s2_=None, op1=None, dt=F32):
+        def ts(name, in0, s1, op0, s2=None, op1=None, dt=F32):
             o = const.tile([P, 64], dt, name=name)
             if op1 is None:
                 nc.vector.tensor_scalar(out=o[:], in0=in0, scalar1=s1, scalar2=None, op0=op0)
             else:
                 nc.vector.tensor_scalar(
-                    out=o[:], in0=in0, scalar1=s1, scalar2=s2_, op0=op0, op1=op1
+                    out=o[:], in0=in0, scalar1=s1, scalar2=s2, op0=op0, op1=op1
                 )
             return o[:]
 
@@ -138,23 +190,46 @@ def tile_groupedstelinear_t_kernel(tc, x, weight_logits, raw_scales, out):
         bp = tt("bp", bl, rp, ALU.mult)
         q = tt("q", at, bt, ALU.add)
         pp = tt("pp", ap, bp, ALU.add)
+
+        presort(0, "s")
+        transpose_x(0)
+        presort(1, "s")
+        transpose_x(1)
+        evac_x(0, "s")
+        quant_x(0, 0, 1)
         rq = rcp("rq", q)
-        half_sign(0)
+        presort(2, "s")
+        transpose_x(2)
+        evac_x(1, "s")
+        quant_x(0, 1, 1)
         z = stt("z", pp, 2.0, ALU.mult, rq, ALU.mult)
-        half_sign(1)
+        presort(3, "s")
+        transpose_x(3)
+        evac_x(2, "s")
+        quant_x(0, 2, 1)
         zz = tt("zz", z, z, ALU.mult)
         m = stt("m", v, 0.0, ALU.max, z, ALU.add)
+        evac_x(3, "s")
+        quant_x(0, 3, 1)
         f1 = ts("f1", zz, AT_ALPHA, ALU.add)
         f2 = stt("f2", zz, AT_BETA, ALU.add, zz, ALU.mult)
         g1 = stt("g1", zz, AT_B1, ALU.add, zz, ALU.mult)
         zw = tt("zw", z, zz, ALU.mult)
+        for i in range(4):
+            presort(4 + i, "s")
+            transpose_x(4 + i)
+            if i > 0:
+                evac_x(4 + i - 1, "s")
+        evac_x(7, "s")
         dm = stt("dm", f2, AT_GAMMA, ALU.add, f1, ALU.mult)
         g2 = stt("g2", g1, AT_B0, ALU.add, zw, ALU.mult)
+        half_sign(0)
         ru = rcp("ru", dm)
-        half_sign(2)
+        half_sign(1)
         corr = stt("corr", g2, AT_KAPPA, ALU.mult, ru, ALU.mult)
-        half_sign(3)
+        half_sign(2)
         sc = stt("sc", corr, 1e-6, ALU.add, m, ALU.add)
+        half_sign(3)
 
         wgrp = const.tile([P, 2, O * 4], BF16, name="wgrp", align_bytes=64)
         wcod = const.tile([P, 2, O], U32, name="wcod", align_bytes=64)
@@ -163,29 +238,35 @@ def tile_groupedstelinear_t_kernel(tc, x, weight_logits, raw_scales, out):
 
         def build_w(t):
             ws = wsp.tile([P, K], BF16, name="ws", tag="ws")
+            wsv = ws[:].rearrange("p (g u a r) -> p g u a r", g=2, u=2, a=4)
             for grp in range(8):
+                g, a = divmod(grp, 4)
                 nc.vector.tensor_scalar(
-                    out=ws[:, grp * P : (grp + 1) * P],
-                    in0=hs[t][:, grp * P : (grp + 1) * P],
+                    out=wsv[:, g, :, a, :],
+                    in0=hs[t][:, grp * P : (grp + 1) * P].rearrange("p (u r) -> p u r", u=2),
                     scalar1=2.0,
                     scalar2=sc[:, t * 8 + grp : t * 8 + grp + 1],
                     op0=ALU.mult,
                     op1=ALU.mult,
                 )
             wt[t] = psum.tile([P, 8, P], BF16, name="wt", tag="bank")
-            for g in range(2):
-                for j in range(4):
-                    nc.tensor.transpose(
-                        wt[t][:, 4 * g + j, :],
-                        ws[:, 512 * g + j : 512 * g + 512 : 4],
-                        ident_b[:],
+            for gu in range(4):
+                for e in range(2):
+                    nc.tensor.matmul(
+                        out=wt[t][:, 2 * gu + e, :],
+                        lhsT=ws[:, 256 * gu + e : 256 * gu + 256 : 2],
+                        rhs=ident_b[:],
+                        start=True,
+                        stop=True,
                     )
 
-        def evac_w(t):
-            nc.scalar.copy(
-                out=wgrp[:].rearrange("p g (o t) -> p g o t", t=4)[:, :, t * P : (t + 1) * P, :],
-                in_=wt[t][:].rearrange("p (g t) o -> p g o t", g=2),
-            )
+        def evac_w(t, eng):
+            dst = wgrp[:].rearrange("p g (o t) -> p g o t", t=4)[:, :, t * P : (t + 1) * P, :]
+            src = wt[t][:].rearrange("p (g t) o -> p g o t", g=2)
+            if eng == "s":
+                nc.scalar.copy(out=dst, in_=src)
+            else:
+                nc.vector.tensor_copy(out=dst, in_=src)
 
         def quant_w(j):
             for g in range(2):
@@ -195,66 +276,35 @@ def tile_groupedstelinear_t_kernel(tc, x, weight_logits, raw_scales, out):
                     in_=wgrp[:, g, 1024 * j : 1024 * j + 1024],
                 )
 
-        xs = {}
-        xt = {}
-        xg = {}
-        xc = {}
-        xp = {}
+        ost = {}
 
-        def presort(c):
-            xs[c] = xsp.tile([P, CH, K], BF16, name="xs", tag="xs")
-            nc.vector.tensor_copy(
-                out=xs[c][:].rearrange("p i k -> p (i k)").bitcast(F32).rearrange(
-                    "p (m u q) -> p m u q", u=2, q=P
-                ),
-                in_=xraw[c][:].rearrange("p i k -> p (i k)").bitcast(F32).rearrange(
-                    "p (m q u) -> p m u q", u=2, q=P
-                ),
-            )
-
-        def transpose_x(c, direct=False):
-            for i in range(CH):
-                xt[c, i] = psum.tile([P, 4, P], F32, name="xt", tag="bank")
-                if direct:
-                    words = xraw[c][:, i, :].bitcast(F32)
-                    for j in range(4):
-                        g, u = divmod(j, 2)
-                        nc.tensor.transpose(
-                            xt[c, i][:, j, :],
-                            words[:, 256 * g + u : 256 * g + 256 : 2],
-                            ident_f[:],
+        def multiply(c, halves):
+            for h in halves:
+                for i in range(CH):
+                    t = CH * c + i
+                    if h == halves[0] and len(halves) == 2 and i % 2 == 0:
+                        ost[t // 2] = osp.tile([P, 2, O], F32, name="ost", tag="ost")
+                    acc = psum.tile([P, 512], F32, name="acc", tag="bank")
+                    for g in range(2):
+                        col = (2 * i + g) * P
+                        nc.tensor.matmul_mx(
+                            out=acc[:],
+                            lhsT=xc[c][:, col : col + P].bitcast(FP8X4),
+                            lhsT_scale=xp[c][:, col : col + P],
+                            rhs=wcod[:, g, 512 * h : 512 * h + 512].bitcast(FP8X4),
+                            rhs_scale=wpla[:, g, 512 * h : 512 * h + 512],
+                            start=(g == 0),
+                            stop=(g == 1),
                         )
-                else:
-                    words = xs[c][:, i, :].bitcast(F32)
-                    for j in range(4):
-                        nc.tensor.transpose(
-                            xt[c, i][:, j, :], words[:, P * j : P * (j + 1)], ident_f[:]
-                        )
+                    nc.scalar.copy(out=ost[t // 2][:, t % 2, 512 * h : 512 * h + 512], in_=acc[:])
+                    if h == 1:
+                        store(t)
 
-        def evac_x(c, eng):
-            xg[c] = xgp.tile([P, CH, K], BF16, name="xg", tag="xg", align_bytes=64)
+        def multiply_by_tile(c):
             for i in range(CH):
-                dst = xg[c][:, i, :].bitcast(F32).rearrange("p (g o u) -> p g o u", g=2, u=2)
-                src = xt[c, i][:].rearrange("p (g u) o -> p g o u", u=2)
-                if eng == "s":
-                    nc.scalar.copy(out=dst, in_=src)
-                else:
-                    nc.vector.tensor_copy(out=dst, in_=src)
-
-        def quant_x(c):
-            xc[c] = xcp.tile([P, CH * 256], U32, name="xc", tag="xc", align_bytes=64)
-            xp[c] = xcp.tile([P, CH * 256], U8, name="xp", tag="xp", align_bytes=64)
-            nc.vector.quantize_mx(
-                out=xc[c][:].bitcast(FP8X4),
-                scales=xp[c][:],
-                in_=xg[c][:].rearrange("p i k -> p (i k)"),
-            )
-
-        def multiply(c):
-            ost = None
-            for i in range(CH):
+                t = CH * c + i
                 if i % 2 == 0:
-                    ost = osp.tile([P, 2, O], F32, name="ost", tag="ost")
+                    ost[t // 2] = osp.tile([P, 2, O], F32, name="ost", tag="ost")
                 for h in range(2):
                     acc = psum.tile([P, 512], F32, name="acc", tag="bank")
                     for g in range(2):
@@ -268,46 +318,44 @@ def tile_groupedstelinear_t_kernel(tc, x, weight_logits, raw_scales, out):
                             start=(g == 0),
                             stop=(g == 1),
                         )
-                    nc.scalar.copy(out=ost[:, i % 2, 512 * h : 512 * h + 512], in_=acc[:])
-                t = CH * c + i
-                if c == NCH - 1 and i >= 2:
-                    nc.sync.dma_start(out=ov[:, t : t + 1, :], in_=ost[:, i % 2 : i % 2 + 1, :])
-                elif i % 2 == 1:
-                    nc.sync.dma_start(out=ov[:, t - 1 : t + 1, :], in_=ost[:])
+                    nc.scalar.copy(out=ost[t // 2][:, t % 2, 512 * h : 512 * h + 512], in_=acc[:])
+                store(t)
 
-        transpose_x(0, direct=True)
-        evac_x(0, "s")
-        transpose_x(1, direct=True)
-        evac_x(1, "s")
-        for t in range(4):
+        def store(t):
+            if t >= NT - 2:
+                nc.sync.dma_start(out=ov[:, t : t + 1, :], in_=ost[t // 2][:, t % 2 : t % 2 + 1, :])
+            elif t % 2 == 1:
+                nc.sync.dma_start(out=ov[:, t - 1 : t + 1, :], in_=ost[t // 2][:])
+
+        for t in range(NOT):
             build_w(t)
-            evac_w(t)
-        quant_x(0)
-        half_sign(4)
-        build_w(4)
-        evac_w(4)
-        half_sign(5)
-        build_w(5)
-        evac_w(5)
+            if t + 4 < NOT:
+                half_sign(t + 4)
+            if t < NOT - 1:
+                evac_w(t, "s")
         quant_w(0)
-        half_sign(6)
-        build_w(6)
-        evac_w(6)
-        half_sign(7)
-        build_w(7)
-        evac_w(7)
         quant_w(1)
-        quant_x(1)
+        ost[0] = osp.tile([P, 2, O], F32, name="ost", tag="ost")
+        ost[1] = osp.tile([P, 2, O], F32, name="ost", tag="ost")
+        multiply(0, [0])
+        evac_w(NOT - 1, "v")
         quant_w(2)
-        presort(2)
         quant_w(3)
+        multiply(0, [1])
+        quant_x(1, 0, CH)
 
-        for r in range(NCH):
+        for r in range(1, NCH):
+            if r + 1 < NCH:
+                if r == 1:
+                    for i in range(CH):
+                        presort(CH * 2 + i, "v")
+                for i in range(CH):
+                    transpose_x(CH * (r + 1) + i)
+                for i in range(CH):
+                    evac_x(CH * (r + 1) + i, "v")
             if r + 2 < NCH:
-                transpose_x(r + 2)
-                evac_x(r + 2, "v")
-            if r + 3 < NCH:
-                presort(r + 3)
-            if r + 2 < NCH:
-                quant_x(r + 2)
-            multiply(r)
+                for i in range(CH):
+                    presort(CH * (r + 2) + i, "v")
+            if r + 1 < NCH:
+                quant_x(r + 1, 0, CH)
+            multiply_by_tile(r)

@@ -41,35 +41,31 @@ def tile_groupedstelinear_t_kernel(tc, x, weight_logits, raw_scales, out):
 
     with ExitStack() as ctx:
         const = ctx.enter_context(tc.tile_pool(name="const", bufs=1))
-        hsp = ctx.enter_context(tc.tile_pool(name="hsp", bufs=4))
         wsp = ctx.enter_context(tc.tile_pool(name="wsp", bufs=3))
         xsp = ctx.enter_context(tc.tile_pool(name="xsp", bufs=8))
         xgp = ctx.enter_context(tc.tile_pool(name="xgp", bufs=2))
         xcp = ctx.enter_context(tc.tile_pool(name="xcp", bufs=3))
-        osp = ctx.enter_context(tc.tile_pool(name="osp", bufs=6))
+        osp = ctx.enter_context(tc.tile_pool(name="osp", bufs=4))
         psum = ctx.enter_context(tc.psum_pool(name="psum", bufs=8))
         ctx.enter_context(tc.manual_schedule())
 
         sraw = const.tile([P, NOT, 8], BF16, name="sraw")
         nc.sync.dma_start(out=sraw[:], in_=sv)
-        wraw = [const.tile([P, 2, K], BF16, name="wraw%d" % j) for j in range(4)]
         xraw = {}
 
         def load_x(first, count):
-            t = const.tile([P, count, K], BF16, name="xraw%d" % first)
-            nc.sync.dma_start(out=t[:], in_=xv[:, first : first + count, :])
+            tl = const.tile([P, count, K], BF16, name="xraw%d" % first)
+            nc.sync.dma_start(out=tl[:], in_=xv[:, first : first + count, :])
             for i in range(count):
-                xraw[first + i] = t[:, i, :]
-
-        def load_w(j):
-            nc.sync.dma_start(out=wraw[j][:], in_=wv[:, 2 * j : 2 * j + 2, :])
+                xraw[first + i] = tl[:, i, :]
 
         for i in range(4):
             load_x(i, 1)
         load_x(4, 2)
         load_x(6, 2)
-        for j in range(4):
-            load_w(j)
+        wsg = [const.tile([P, K], BF16, name="wsg%d" % j) for j in range(NOT)]
+        for j in range(NOT):
+            nc.sync.dma_start(out=wsg[j][:], in_=wv[:, j, :])
         for c in range(2, NCH):
             load_x(CH * c, CH)
 
@@ -110,31 +106,44 @@ def tile_groupedstelinear_t_kernel(tc, x, weight_logits, raw_scales, out):
 
         def evac_x(t, eng):
             c, i = divmod(t, CH)
-            if i == 0:
-                xg[c] = xgp.tile([P, CH, K], BF16, name="xg", tag="xg", align_bytes=64)
-            dst = xg[c][:, i, :].bitcast(F32).rearrange("p (g o u) -> p g o u", g=2, u=2)
+            if c == 0:
+                xg[t] = const.tile([P, K], BF16, name="xg0_%d" % i, align_bytes=64)
+                grouped = xg[t][:]
+            else:
+                if i == 0:
+                    xg[-c] = xgp.tile([P, CH, K], BF16, name="xg", tag="xg", align_bytes=64)
+                grouped = xg[-c][:, i, :]
+            dst = grouped.bitcast(F32).rearrange("p (g o u) -> p g o u", g=2, u=2)
             src = xt[t][:].rearrange("p (g u) o -> p g o u", u=2)
             if eng == "s":
                 nc.scalar.copy(out=dst, in_=src)
             else:
                 nc.vector.tensor_copy(out=dst, in_=src)
 
-        def quant_x(c, first, count):
-            if first == 0:
-                xc[c] = xcp.tile([P, CH * 256], U32, name="xc", tag="xc", align_bytes=64)
-                xp[c] = xcp.tile([P, CH * 256], U8, name="xp", tag="xp", align_bytes=64)
+        def codes_x(c):
+            xc[c] = xcp.tile([P, CH * 256], U32, name="xc", tag="xc", align_bytes=64)
+            xp[c] = xcp.tile([P, CH * 256], U8, name="xp", tag="xp", align_bytes=64)
+
+        def quant_x0(i):
+            if i == 0:
+                codes_x(0)
             nc.vector.quantize_mx(
-                out=xc[c][:, 256 * first : 256 * (first + count)].bitcast(FP8X4),
-                scales=xp[c][:, 256 * first : 256 * (first + count)],
-                in_=xg[c][:, first : first + count, :].rearrange("p i k -> p (i k)"),
+                out=xc[0][:, 256 * i : 256 * (i + 1)].bitcast(FP8X4),
+                scales=xp[0][:, 256 * i : 256 * (i + 1)],
+                in_=xg[i][:],
             )
 
-        hs = {}
+        def quant_x(c):
+            codes_x(c)
+            nc.vector.quantize_mx(
+                out=xc[c][:].bitcast(FP8X4),
+                scales=xp[c][:],
+                in_=xg[-c][:].rearrange("p i k -> p (i k)"),
+            )
 
         def half_sign(t):
-            hs[t] = hsp.tile([P, K], BF16, name="hs", tag="hs")
             nc.vector.tensor_scalar(
-                out=hs[t][:], in0=wraw[t // 2][:, t % 2, :], scalar1=0.0, scalar2=0.5,
+                out=wsg[t][:], in0=wsg[t][:], scalar1=0.0, scalar2=0.5,
                 op0=ALU.is_ge, op1=ALU.subtract,
             )
 
@@ -170,6 +179,19 @@ def tile_groupedstelinear_t_kernel(tc, x, weight_logits, raw_scales, out):
             nc.vector.reciprocal(out=o[:], in_=in_)
             return o[:]
 
+        presort(0, "s")
+        transpose_x(0)
+        presort(1, "s")
+        transpose_x(1)
+        evac_x(0, "s")
+        presort(2, "s")
+        transpose_x(2)
+        evac_x(1, "s")
+        presort(3, "s")
+        transpose_x(3)
+        evac_x(2, "s")
+        evac_x(3, "s")
+
         na = stt("na", v, -1.0, ALU.mult, v, ALU.min)
         ni = ts("ni", na, LOG2E, ALU.mult, -126.0, ALU.max, dt=I32)
         rh = stt("rh", ni, -LN2HI, ALU.mult, na, ALU.add)
@@ -182,58 +204,51 @@ def tile_groupedstelinear_t_kernel(tc, x, weight_logits, raw_scales, out):
         w = tt("w", r, r, ALU.mult)
         rt = tt("rt", r, t2, ALU.mult)
         rp = tt("rp", r, p2, ALU.mult)
+        quant_x0(0)
         a1 = stt("a1", w, 180.0, ALU.add, w, ALU.mult)
         bl = ts("bl", w, 20.0, ALU.mult, 840.0, ALU.add)
+        presort(4, "v")
+        transpose_x(4)
         at = stt("at", a1, 1680.0, ALU.add, t1, ALU.mult)
         bt = tt("bt", bl, rt, ALU.mult)
         ap = stt("ap", a1, 1680.0, ALU.add, p2, ALU.mult)
         bp = tt("bp", bl, rp, ALU.mult)
+        presort(5, "v")
+        transpose_x(5)
+        evac_x(4, "s")
         q = tt("q", at, bt, ALU.add)
         pp = tt("pp", ap, bp, ALU.add)
-
-        presort(0, "s")
-        transpose_x(0)
-        presort(1, "s")
-        transpose_x(1)
-        evac_x(0, "s")
-        quant_x(0, 0, 1)
+        quant_x0(1)
         rq = rcp("rq", q)
-        presort(2, "s")
-        transpose_x(2)
-        evac_x(1, "s")
-        quant_x(0, 1, 1)
+        presort(6, "v")
+        transpose_x(6)
+        evac_x(5, "s")
         z = stt("z", pp, 2.0, ALU.mult, rq, ALU.mult)
-        presort(3, "s")
-        transpose_x(3)
-        evac_x(2, "s")
-        quant_x(0, 2, 1)
+        quant_x0(2)
         zz = tt("zz", z, z, ALU.mult)
         m = stt("m", v, 0.0, ALU.max, z, ALU.add)
-        evac_x(3, "s")
-        quant_x(0, 3, 1)
+        presort(7, "v")
+        transpose_x(7)
+        evac_x(6, "s")
+        evac_x(7, "s")
         f1 = ts("f1", zz, AT_ALPHA, ALU.add)
         f2 = stt("f2", zz, AT_BETA, ALU.add, zz, ALU.mult)
         g1 = stt("g1", zz, AT_B1, ALU.add, zz, ALU.mult)
         zw = tt("zw", z, zz, ALU.mult)
-        for i in range(4):
-            presort(4 + i, "s")
-            transpose_x(4 + i)
-            if i > 0:
-                evac_x(4 + i - 1, "s")
-        evac_x(7, "s")
+        quant_x0(3)
         dm = stt("dm", f2, AT_GAMMA, ALU.add, f1, ALU.mult)
         g2 = stt("g2", g1, AT_B0, ALU.add, zw, ALU.mult)
         half_sign(0)
         ru = rcp("ru", dm)
         half_sign(1)
-        corr = stt("corr", g2, AT_KAPPA, ALU.mult, ru, ALU.mult)
         half_sign(2)
-        sc = stt("sc", corr, 1e-6, ALU.add, m, ALU.add)
+        corr = stt("corr", g2, AT_KAPPA, ALU.mult, ru, ALU.mult)
         half_sign(3)
+        sc = stt("sc", corr, 1e-6, ALU.add, m, ALU.add)
 
-        wgrp = const.tile([P, 2, O * 4], BF16, name="wgrp", align_bytes=64)
-        wcod = const.tile([P, 2, O], U32, name="wcod", align_bytes=64)
-        wpla = const.tile([P, 2, O], U8, name="wpla", align_bytes=64)
+        wgrp = [const.tile([P, 2, 512], BF16, name="wgrp%d" % t, align_bytes=64) for t in range(NOT)]
+        wcod = [const.tile([P, 2, 512], U32, name="wcod%d" % h, align_bytes=64) for h in range(2)]
+        wpla = [const.tile([P, 2, 512], U8, name="wpla%d" % h, align_bytes=64) for h in range(2)]
         wt = {}
 
         def build_w(t):
@@ -243,7 +258,7 @@ def tile_groupedstelinear_t_kernel(tc, x, weight_logits, raw_scales, out):
                 g, a = divmod(grp, 4)
                 nc.vector.tensor_scalar(
                     out=wsv[:, g, :, a, :],
-                    in0=hs[t][:, grp * P : (grp + 1) * P].rearrange("p (u r) -> p u r", u=2),
+                    in0=wsg[t][:, grp * P : (grp + 1) * P].rearrange("p (u r) -> p u r", u=2),
                     scalar1=2.0,
                     scalar2=sc[:, t * 8 + grp : t * 8 + grp + 1],
                     op0=ALU.mult,
@@ -261,101 +276,121 @@ def tile_groupedstelinear_t_kernel(tc, x, weight_logits, raw_scales, out):
                     )
 
         def evac_w(t, eng):
-            dst = wgrp[:].rearrange("p g (o t) -> p g o t", t=4)[:, :, t * P : (t + 1) * P, :]
+            dst = wgrp[t][:].rearrange("p g (o t) -> p g o t", t=4)
             src = wt[t][:].rearrange("p (g t) o -> p g o t", g=2)
             if eng == "s":
                 nc.scalar.copy(out=dst, in_=src)
             else:
                 nc.vector.tensor_copy(out=dst, in_=src)
 
-        def quant_w(j):
+        def quant_w(t):
+            h, j = divmod(t, 4)
             for g in range(2):
                 nc.vector.quantize_mx(
-                    out=wcod[:, g, 256 * j : 256 * j + 256].bitcast(FP8X4),
-                    scales=wpla[:, g, 256 * j : 256 * j + 256],
-                    in_=wgrp[:, g, 1024 * j : 1024 * j + 1024],
+                    out=wcod[h][:, g, P * j : P * (j + 1)].bitcast(FP8X4),
+                    scales=wpla[h][:, g, P * j : P * (j + 1)],
+                    in_=wgrp[t][:, g, :],
                 )
 
         ost = {}
 
-        def multiply(c, halves):
-            for h in halves:
+        def passes(t, h, eng, dst=None):
+            c, i = divmod(t, CH)
+            acc = psum.tile([P, 512], F32, name="acc", tag="bank")
+            for g in range(2):
+                col = (2 * i + g) * P
+                nc.tensor.matmul_mx(
+                    out=acc[:],
+                    lhsT=xc[c][:, col : col + P].bitcast(FP8X4),
+                    lhsT_scale=xp[c][:, col : col + P],
+                    rhs=wcod[h][:, g, :].bitcast(FP8X4),
+                    rhs_scale=wpla[h][:, g, :],
+                    start=(g == 0),
+                    stop=(g == 1),
+                )
+            if dst is None:
+                dst = ost[t // 2][:, t % 2, 512 * h : 512 * h + 512]
+            if eng == "s":
+                nc.scalar.copy(out=dst, in_=acc[:])
+            else:
+                nc.vector.tensor_copy(out=dst, in_=acc[:])
+
+        def new_ost(t):
+            ost[t // 2] = osp.tile([P, 2, O], F32, name="ost", tag="ost")
+
+        def store_pair(t):
+            nc.sync.dma_start(out=ov[:, t - 1 : t + 1, :], in_=ost[t // 2][:])
+
+
+        build_w(0)
+        evac_w(0, "s")
+        build_w(1)
+        evac_w(1, "s")
+        half_sign(4)
+        build_w(2)
+        evac_w(2, "s")
+        half_sign(5)
+        quant_w(0)
+        build_w(3)
+        evac_w(3, "s")
+        half_sign(6)
+        quant_w(1)
+        build_w(4)
+        evac_w(4, "s")
+        half_sign(7)
+        quant_w(2)
+        build_w(5)
+        evac_w(5, "s")
+        build_w(6)
+        evac_w(6, "s")
+        quant_w(3)
+        build_w(7)
+        evac_w(7, "v")
+        new_ost(0)
+        new_ost(2)
+        for i in range(CH):
+            passes(i, 0, "s")
+        quant_w(4)
+        quant_w(5)
+        quant_w(6)
+        quant_w(7)
+        for i in range(CH):
+            passes(i, 1, "s")
+            if i % 2 == 1:
+                store_pair(i)
+        quant_x(1)
+
+        for i in range(CH):
+            presort(2 * CH + i, "v")
+        for c in range(1, NCH):
+            if c + 1 < NCH:
+                for i in range(CH):
+                    transpose_x(CH * (c + 1) + i)
+                for i in range(CH):
+                    evac_x(CH * (c + 1) + i, "v")
+            if c + 2 < NCH:
+                for i in range(CH):
+                    presort(CH * (c + 2) + i, "v")
+            if c + 1 < NCH:
+                quant_x(c + 1)
+            if c < NCH - 1:
                 for i in range(CH):
                     t = CH * c + i
-                    if h == halves[0] and len(halves) == 2 and i % 2 == 0:
-                        ost[t // 2] = osp.tile([P, 2, O], F32, name="ost", tag="ost")
-                    acc = psum.tile([P, 512], F32, name="acc", tag="bank")
-                    for g in range(2):
-                        col = (2 * i + g) * P
-                        nc.tensor.matmul_mx(
-                            out=acc[:],
-                            lhsT=xc[c][:, col : col + P].bitcast(FP8X4),
-                            lhsT_scale=xp[c][:, col : col + P],
-                            rhs=wcod[:, g, 512 * h : 512 * h + 512].bitcast(FP8X4),
-                            rhs_scale=wpla[:, g, 512 * h : 512 * h + 512],
-                            start=(g == 0),
-                            stop=(g == 1),
-                        )
-                    nc.scalar.copy(out=ost[t // 2][:, t % 2, 512 * h : 512 * h + 512], in_=acc[:])
-                    if h == 1:
-                        store(t)
-
-        def multiply_by_tile(c):
-            for i in range(CH):
-                t = CH * c + i
-                if i % 2 == 0:
-                    ost[t // 2] = osp.tile([P, 2, O], F32, name="ost", tag="ost")
+                    if i % 2 == 0:
+                        new_ost(t)
+                    passes(t, 0, "s")
+                    passes(t, 1, "s")
+                    if i % 2 == 1:
+                        store_pair(t)
+        for i in range(CH):
+            t = CH * (NCH - 1) + i
+            if i < CH - 1:
+                whole = const.tile([P, 1, O], F32, name="olast%d" % i)
+                passes(t, 0, "s", whole[:, 0, 0:512])
+                passes(t, 1, "v", whole[:, 0, 512:O])
+                nc.sync.dma_start(out=ov[:, t : t + 1, :], in_=whole[:])
+            else:
                 for h in range(2):
-                    acc = psum.tile([P, 512], F32, name="acc", tag="bank")
-                    for g in range(2):
-                        col = (2 * i + g) * P
-                        nc.tensor.matmul_mx(
-                            out=acc[:],
-                            lhsT=xc[c][:, col : col + P].bitcast(FP8X4),
-                            lhsT_scale=xp[c][:, col : col + P],
-                            rhs=wcod[:, g, 512 * h : 512 * h + 512].bitcast(FP8X4),
-                            rhs_scale=wpla[:, g, 512 * h : 512 * h + 512],
-                            start=(g == 0),
-                            stop=(g == 1),
-                        )
-                    nc.scalar.copy(out=ost[t // 2][:, t % 2, 512 * h : 512 * h + 512], in_=acc[:])
-                store(t)
-
-        def store(t):
-            if t >= NT - 2:
-                nc.sync.dma_start(out=ov[:, t : t + 1, :], in_=ost[t // 2][:, t % 2 : t % 2 + 1, :])
-            elif t % 2 == 1:
-                nc.sync.dma_start(out=ov[:, t - 1 : t + 1, :], in_=ost[t // 2][:])
-
-        for t in range(NOT):
-            build_w(t)
-            if t + 4 < NOT:
-                half_sign(t + 4)
-            if t < NOT - 1:
-                evac_w(t, "s")
-        quant_w(0)
-        quant_w(1)
-        ost[0] = osp.tile([P, 2, O], F32, name="ost", tag="ost")
-        ost[1] = osp.tile([P, 2, O], F32, name="ost", tag="ost")
-        multiply(0, [0])
-        evac_w(NOT - 1, "v")
-        quant_w(2)
-        quant_w(3)
-        multiply(0, [1])
-        quant_x(1, 0, CH)
-
-        for r in range(1, NCH):
-            if r + 1 < NCH:
-                if r == 1:
-                    for i in range(CH):
-                        presort(CH * 2 + i, "v")
-                for i in range(CH):
-                    transpose_x(CH * (r + 1) + i)
-                for i in range(CH):
-                    evac_x(CH * (r + 1) + i, "v")
-            if r + 2 < NCH:
-                for i in range(CH):
-                    presort(CH * (r + 2) + i, "v")
-            if r + 1 < NCH:
-                quant_x(r + 1, 0, CH)
-            multiply_by_tile(r)
+                    part = const.tile([P, 1, 512], F32, name="opart%d" % h)
+                    passes(t, h, "sv"[h], part[:, 0, :])
+                    nc.sync.dma_start(out=ov[:, t : t + 1, 512 * h : 512 * h + 512], in_=part[:])

@@ -47,7 +47,6 @@ def tile_groupedstelinear_t_kernel(tc, x, weight_logits, raw_scales, out):
         xcp = ctx.enter_context(tc.tile_pool(name="xcp", bufs=3))
         osp = ctx.enter_context(tc.tile_pool(name="osp", bufs=4))
         psum = ctx.enter_context(tc.psum_pool(name="psum", bufs=8))
-        ctx.enter_context(tc.manual_schedule())
 
         sraw = const.tile([P, NOT, 8], BF16, name="sraw")
         nc.sync.dma_start(out=sraw[:], in_=sv)

@@ -47,6 +47,7 @@ def tile_groupedstelinear_t_kernel(tc, x, weight_logits, raw_scales, out):
         xcp = ctx.enter_context(tc.tile_pool(name="xcp", bufs=3))
         osp = ctx.enter_context(tc.tile_pool(name="osp", bufs=4))
         psum = ctx.enter_context(tc.psum_pool(name="psum", bufs=8))
+        ctx.enter_context(tc.manual_schedule())
 
         sraw = const.tile([P, NOT, 8], BF16, name="sraw")
         nc.sync.dma_start(out=sraw[:], in_=sv)
@@ -321,29 +322,16 @@ def tile_groupedstelinear_t_kernel(tc, x, weight_logits, raw_scales, out):
             nc.sync.dma_start(out=ov[:, t - 1 : t + 1, :], in_=ost[t // 2][:])
 
 
-        build_w(0)
-        evac_w(0, "s")
-        build_w(1)
-        evac_w(1, "s")
-        half_sign(4)
-        build_w(2)
-        evac_w(2, "s")
-        half_sign(5)
+        for t in range(NOT):
+            if t + 4 < NOT:
+                half_sign(t + 4)
+            build_w(t)
+            if t < NOT - 1:
+                evac_w(t, "s")
         quant_w(0)
-        build_w(3)
-        evac_w(3, "s")
-        half_sign(6)
         quant_w(1)
-        build_w(4)
-        evac_w(4, "s")
-        half_sign(7)
         quant_w(2)
-        build_w(5)
-        evac_w(5, "s")
-        build_w(6)
-        evac_w(6, "s")
         quant_w(3)
-        build_w(7)
         evac_w(7, "v")
         new_ost(0)
         new_ost(2)

@@ -7,21 +7,11 @@ FLOPS = 2 * 4096 * 1024 * 1024
 
 BF16 = mybir.dt.bfloat16
 F32 = mybir.dt.float32
-I32 = mybir.dt.int32
 U32 = mybir.dt.uint32
 U8 = mybir.dt.uint8
 FP8X4 = mybir.dt.float8_e4m3fn_x4
 ALU = mybir.AluOpType
-
-LOG2E = 1.4426950408889634
-LN2HI = 0.693359375
-LN2LO = 0.6931471805599453 - 0.693359375
-AT_ALPHA = -4.440468600468879
-AT_BETA = -31.55953139953112
-AT_GAMMA = 176.6608917748704
-AT_B1 = 4.0 * -45738.0 / 8721.0
-AT_B0 = 16.0 * 45045.0 / 8721.0
-AT_KAPPA = 8721.0 / -11025.0
+ACT = mybir.ActivationFunctionType
 
 P = 128
 K = 1024
@@ -41,7 +31,6 @@ def tile_groupedstelinear_t_kernel(tc, x, weight_logits, raw_scales, out):
 
     with ExitStack() as ctx:
         const = ctx.enter_context(tc.tile_pool(name="const", bufs=1))
-        wsp = ctx.enter_context(tc.tile_pool(name="wsp", bufs=3))
         xsp = ctx.enter_context(tc.tile_pool(name="xsp", bufs=8))
         xgp = ctx.enter_context(tc.tile_pool(name="xgp", bufs=2))
         xcp = ctx.enter_context(tc.tile_pool(name="xcp", bufs=3))
@@ -52,6 +41,7 @@ def tile_groupedstelinear_t_kernel(tc, x, weight_logits, raw_scales, out):
         sraw = const.tile([P, NOT, 8], BF16, name="sraw")
         nc.sync.dma_start(out=sraw[:], in_=sv)
         xraw = {}
+        wraw = {}
 
         def load_x(first, count):
             tl = const.tile([P, count, K], BF16, name="xraw%d" % first)
@@ -59,20 +49,24 @@ def tile_groupedstelinear_t_kernel(tc, x, weight_logits, raw_scales, out):
             for i in range(count):
                 xraw[first + i] = tl[:, i, :]
 
+        def load_w(t):
+            tl = const.tile([P, K], BF16, name="wraw%d" % t)
+            nc.sync.dma_start(out=tl[:], in_=wv[:, t, :])
+            wraw[t] = tl
+
+        for t in range(4):
+            load_w(t)
         for i in range(4):
             load_x(i, 1)
+        for t in range(4, NOT):
+            load_w(t)
         load_x(4, 2)
         load_x(6, 2)
-        wsg = [const.tile([P, K], BF16, name="wsg%d" % j) for j in range(NOT)]
-        for j in range(NOT):
-            nc.sync.dma_start(out=wsg[j][:], in_=wv[:, j, :])
         for c in range(2, NCH):
             load_x(CH * c, CH)
 
         ident_f = const.tile([P, P], F32, name="ident_f")
         make_identity(nc, ident_f[:])
-        ident_b = const.tile([P, P], BF16, name="ident_b")
-        make_identity(nc, ident_b[:])
 
         xs = {}
         xt = {}
@@ -80,29 +74,23 @@ def tile_groupedstelinear_t_kernel(tc, x, weight_logits, raw_scales, out):
         xc = {}
         xp = {}
 
-        def presort(t, eng):
+        def presort(t):
             xs[t] = xsp.tile([P, K], BF16, name="xs", tag="xs")
-            if eng == "s":
-                for g in range(2):
-                    nc.scalar.copy(
-                        out=xs[t][:, 512 * g : 512 * g + 512].bitcast(F32).rearrange(
-                            "p (u a r) -> p u a r", u=2, a=4
-                        ),
-                        in_=xraw[t][:, 512 * g : 512 * g + 512].bitcast(F32).rearrange(
-                            "p (a u r) -> p u a r", u=2, a=4
-                        ),
-                    )
-            else:
-                nc.vector.tensor_copy(
-                    out=xs[t][:].rearrange("p (g u a r) -> p g u a r", g=2, u=2, a=4),
-                    in_=xraw[t].rearrange("p (g a u r) -> p g u a r", g=2, u=2, a=4),
-                )
+            nc.vector.tensor_copy(
+                out=xs[t][:].bitcast(F32).rearrange("p (g u q) -> p g u q", g=2, u=2),
+                in_=xraw[t].bitcast(F32).rearrange("p (g q u) -> p g u q", g=2, u=2),
+            )
 
-        def transpose_x(t):
+        def transpose_x(t, direct):
             xt[t] = psum.tile([P, 4, P], F32, name="xt", tag="bank")
-            words = xs[t][:].bitcast(F32)
+            words = (xraw[t] if direct else xs[t][:]).bitcast(F32)
             for j in range(4):
-                nc.tensor.transpose(xt[t][:, j, :], words[:, P * j : P * (j + 1)], ident_f[:])
+                g, u = divmod(j, 2)
+                if direct:
+                    cols = words[:, 256 * g + u : 256 * (g + 1) : 2]
+                else:
+                    cols = words[:, P * j : P * (j + 1)]
+                nc.tensor.transpose(xt[t][:, j, :], cols, ident_f[:])
 
         def evac_x(t, eng):
             c, i = divmod(t, CH)
@@ -110,7 +98,7 @@ def tile_groupedstelinear_t_kernel(tc, x, weight_logits, raw_scales, out):
                 xg[t] = const.tile([P, K], BF16, name="xg0_%d" % i, align_bytes=64)
                 grouped = xg[t][:]
             else:
-                if i == 0:
+                if -c not in xg:
                     xg[-c] = xgp.tile([P, CH, K], BF16, name="xg", tag="xg", align_bytes=64)
                 grouped = xg[-c][:, i, :]
             dst = grouped.bitcast(F32).rearrange("p (g o u) -> p g o u", g=2, u=2)
@@ -133,6 +121,16 @@ def tile_groupedstelinear_t_kernel(tc, x, weight_logits, raw_scales, out):
                 in_=xg[i][:],
             )
 
+        def quant_x1(t):
+            c, i = divmod(t, CH)
+            if i == 0:
+                codes_x(c)
+            nc.vector.quantize_mx(
+                out=xc[c][:, 256 * i : 256 * (i + 1)].bitcast(FP8X4),
+                scales=xp[c][:, 256 * i : 256 * (i + 1)],
+                in_=xg[-c][:, i, :],
+            )
+
         def quant_x(c):
             codes_x(c)
             nc.vector.quantize_mx(
@@ -141,143 +139,47 @@ def tile_groupedstelinear_t_kernel(tc, x, weight_logits, raw_scales, out):
                 in_=xg[-c][:].rearrange("p i k -> p (i k)"),
             )
 
+        hs = {}
+
         def half_sign(t):
-            nc.vector.tensor_scalar(
-                out=wsg[t][:], in0=wsg[t][:], scalar1=0.0, scalar2=0.5,
-                op0=ALU.is_ge, op1=ALU.subtract,
-            )
-
-        v = sraw[:].rearrange("p t g -> p (t g)")
-
-        def f32tile(name):
-            return const.tile([P, 64], F32, name=name)
-
-        def stt(name, in0, scalar, op0, in1, op1):
-            o = f32tile(name)
-            nc.vector.scalar_tensor_tensor(
-                out=o[:], in0=in0, scalar=scalar, in1=in1, op0=op0, op1=op1
-            )
-            return o[:]
-
-        def ts(name, in0, s1, op0, s2=None, op1=None, dt=F32):
-            o = const.tile([P, 64], dt, name=name)
-            if op1 is None:
-                nc.vector.tensor_scalar(out=o[:], in0=in0, scalar1=s1, scalar2=None, op0=op0)
-            else:
+            hs[t] = const.tile([P, K], BF16, name="hs%d" % t)
+            for g in range(2):
                 nc.vector.tensor_scalar(
-                    out=o[:], in0=in0, scalar1=s1, scalar2=s2, op0=op0, op1=op1
+                    out=hs[t][:, 512 * g : 512 * g + 512].rearrange("p (u q e) -> p u q e", u=2, e=2),
+                    in0=wraw[t][:, 512 * g : 512 * g + 512].rearrange("p (q u e) -> p u q e", u=2, e=2),
+                    scalar1=0.0, scalar2=0.5,
+                    op0=ALU.is_ge, op1=ALU.subtract,
                 )
-            return o[:]
 
-        def tt(name, in0, in1, op):
-            o = f32tile(name)
-            nc.vector.tensor_tensor(out=o[:], in0=in0, in1=in1, op=op)
-            return o[:]
-
-        def rcp(name, in_):
-            o = f32tile(name)
-            nc.vector.reciprocal(out=o[:], in_=in_)
-            return o[:]
-
-        presort(0, "s")
-        transpose_x(0)
-        presort(1, "s")
-        transpose_x(1)
-        evac_x(0, "s")
-        presort(2, "s")
-        transpose_x(2)
-        evac_x(1, "s")
-        presort(3, "s")
-        transpose_x(3)
-        evac_x(2, "s")
-        evac_x(3, "s")
-
-        na = stt("na", v, -1.0, ALU.mult, v, ALU.min)
-        ni = ts("ni", na, LOG2E, ALU.mult, -126.0, ALU.max, dt=I32)
-        rh = stt("rh", ni, -LN2HI, ALU.mult, na, ALU.add)
-        lo = ts("lo", ni, -LN2LO, ALU.mult)
-        pw = ts("pw", ni, 127.0, ALU.add, 8388608.0, ALU.mult, dt=I32)
-        p2 = pw.bitcast(F32)
-        r = stt("r", rh, -1.0, ALU.max, lo, ALU.add)
-        t1 = ts("t1", p2, 2.0, ALU.add)
-        t2 = ts("t2", p2, 2.0, ALU.subtract)
-        w = tt("w", r, r, ALU.mult)
-        rt = tt("rt", r, t2, ALU.mult)
-        rp = tt("rp", r, p2, ALU.mult)
-        quant_x0(0)
-        a1 = stt("a1", w, 180.0, ALU.add, w, ALU.mult)
-        bl = ts("bl", w, 20.0, ALU.mult, 840.0, ALU.add)
-        presort(4, "v")
-        transpose_x(4)
-        at = stt("at", a1, 1680.0, ALU.add, t1, ALU.mult)
-        bt = tt("bt", bl, rt, ALU.mult)
-        ap = stt("ap", a1, 1680.0, ALU.add, p2, ALU.mult)
-        bp = tt("bp", bl, rp, ALU.mult)
-        presort(5, "v")
-        transpose_x(5)
-        evac_x(4, "s")
-        q = tt("q", at, bt, ALU.add)
-        pp = tt("pp", ap, bp, ALU.add)
-        quant_x0(1)
-        rq = rcp("rq", q)
-        presort(6, "v")
-        transpose_x(6)
-        evac_x(5, "s")
-        z = stt("z", pp, 2.0, ALU.mult, rq, ALU.mult)
-        quant_x0(2)
-        zz = tt("zz", z, z, ALU.mult)
-        m = stt("m", v, 0.0, ALU.max, z, ALU.add)
-        presort(7, "v")
-        transpose_x(7)
-        evac_x(6, "s")
-        evac_x(7, "s")
-        f1 = ts("f1", zz, AT_ALPHA, ALU.add)
-        f2 = stt("f2", zz, AT_BETA, ALU.add, zz, ALU.mult)
-        g1 = stt("g1", zz, AT_B1, ALU.add, zz, ALU.mult)
-        zw = tt("zw", z, zz, ALU.mult)
-        quant_x0(3)
-        dm = stt("dm", f2, AT_GAMMA, ALU.add, f1, ALU.mult)
-        g2 = stt("g2", g1, AT_B0, ALU.add, zw, ALU.mult)
-        half_sign(0)
-        ru = rcp("ru", dm)
-        half_sign(1)
-        half_sign(2)
-        corr = stt("corr", g2, AT_KAPPA, ALU.mult, ru, ALU.mult)
-        half_sign(3)
-        sc = stt("sc", corr, 1e-6, ALU.add, m, ALU.add)
+        def scale_w(t):
+            v = hs[t][:].rearrange("p (g u a r) -> p g u a r", g=2, u=2, a=4)
+            for grp in range(8):
+                g, a = divmod(grp, 4)
+                nc.vector.tensor_scalar(
+                    out=v[:, g, :, a, :],
+                    in0=v[:, g, :, a, :],
+                    scalar1=2.0,
+                    scalar2=sc[:, t * 8 + grp : t * 8 + grp + 1],
+                    op0=ALU.mult,
+                    op1=ALU.mult,
+                )
 
         wgrp = [const.tile([P, 2, 512], BF16, name="wgrp%d" % t, align_bytes=64) for t in range(NOT)]
         wcod = [const.tile([P, 2, 512], U32, name="wcod%d" % h, align_bytes=64) for h in range(2)]
         wpla = [const.tile([P, 2, 512], U8, name="wpla%d" % h, align_bytes=64) for h in range(2)]
         wt = {}
 
-        def build_w(t):
-            ws = wsp.tile([P, K], BF16, name="ws", tag="ws")
-            wsv = ws[:].rearrange("p (g u a r) -> p g u a r", g=2, u=2, a=4)
-            for grp in range(8):
-                g, a = divmod(grp, 4)
-                nc.vector.tensor_scalar(
-                    out=wsv[:, g, :, a, :],
-                    in0=wsg[t][:, grp * P : (grp + 1) * P].rearrange("p (u r) -> p u r", u=2),
-                    scalar1=2.0,
-                    scalar2=sc[:, t * 8 + grp : t * 8 + grp + 1],
-                    op0=ALU.mult,
-                    op1=ALU.mult,
-                )
-            wt[t] = psum.tile([P, 8, P], BF16, name="wt", tag="bank")
-            for gu in range(4):
-                for e in range(2):
-                    nc.tensor.matmul(
-                        out=wt[t][:, 2 * gu + e, :],
-                        lhsT=ws[:, 256 * gu + e : 256 * gu + 256 : 2],
-                        rhs=ident_b[:],
-                        start=True,
-                        stop=True,
-                    )
+        def planes_w(t):
+            wt[t] = psum.tile([P, 4, P], F32, name="wt", tag="bank")
+            words = hs[t][:].bitcast(F32)
+            for j in range(4):
+                nc.tensor.transpose(wt[t][:, j, :], words[:, P * j : P * (j + 1)], ident_f[:])
 
         def evac_w(t, eng):
-            dst = wgrp[t][:].rearrange("p g (o t) -> p g o t", t=4)
-            src = wt[t][:].rearrange("p (g t) o -> p g o t", g=2)
+            dst = wgrp[t][:].rearrange("p g c -> p (g c)").bitcast(F32).rearrange(
+                "p (g o u) -> p g o u", g=2, u=2
+            )
+            src = wt[t][:].rearrange("p (g u) o -> p g o u", u=2)
             if eng == "s":
                 nc.scalar.copy(out=dst, in_=src)
             else:
@@ -294,13 +196,15 @@ def tile_groupedstelinear_t_kernel(tc, x, weight_logits, raw_scales, out):
 
         ost = {}
 
-        def passes(t, h, eng, dst=None):
+        acc = {}
+
+        def passes(t, h):
             c, i = divmod(t, CH)
-            acc = psum.tile([P, 512], F32, name="acc", tag="bank")
+            acc[t, h] = psum.tile([P, 512], F32, name="acc", tag="bank")
             for g in range(2):
                 col = (2 * i + g) * P
                 nc.tensor.matmul_mx(
-                    out=acc[:],
+                    out=acc[t, h][:],
                     lhsT=xc[c][:, col : col + P].bitcast(FP8X4),
                     lhsT_scale=xp[c][:, col : col + P],
                     rhs=wcod[h][:, g, :].bitcast(FP8X4),
@@ -308,76 +212,168 @@ def tile_groupedstelinear_t_kernel(tc, x, weight_logits, raw_scales, out):
                     start=(g == 0),
                     stop=(g == 1),
                 )
+
+        def evac_o(t, h, eng, dst=None):
             if dst is None:
+                if t // 2 not in ost:
+                    ost[t // 2] = osp.tile([P, 2, O], F32, name="ost", tag="ost")
                 dst = ost[t // 2][:, t % 2, 512 * h : 512 * h + 512]
             if eng == "s":
-                nc.scalar.copy(out=dst, in_=acc[:])
+                nc.scalar.copy(out=dst, in_=acc[t, h][:])
             else:
-                nc.vector.tensor_copy(out=dst, in_=acc[:])
-
-        def new_ost(t):
-            ost[t // 2] = osp.tile([P, 2, O], F32, name="ost", tag="ost")
+                nc.vector.tensor_copy(out=dst, in_=acc[t, h][:])
 
         def store_pair(t):
             nc.sync.dma_start(out=ov[:, t - 1 : t + 1, :], in_=ost[t // 2][:])
 
+        def store_one(t):
+            nc.sync.dma_start(out=ov[:, t : t + 1, :], in_=ost[t // 2][:, t % 2 : t % 2 + 1, :])
 
-        for t in range(NOT):
-            if t + 4 < NOT:
-                half_sign(t + 4)
-            build_w(t)
-            if t < NOT - 1:
-                evac_w(t, "s")
+        v = sraw[:].rearrange("p t g -> p (t g)")
+        names = ("av", "z", "ln", "m", "tz", "e", "me", "sc")
+        s = {n: const.tile([P, 64], F32, name=n) for n in names}
+        nc.scalar.activation(out=s["av"][:], in_=v, func=ACT.Abs)
+        nc.scalar.activation(out=s["z"][:], in_=s["av"][:], func=ACT.Exp, scale=-1.0)
+        nc.scalar.activation(out=s["ln"][:], in_=s["z"][:], func=ACT.Ln, bias=1.0)
+        nc.vector.tensor_scalar(out=s["m"][:], in0=v, scalar1=0.0, scalar2=None, op0=ALU.max)
+        half_sign(0)
+        nc.vector.tensor_scalar(
+            out=s["tz"][:], in0=s["z"][:], scalar1=1.0, scalar2=1.0, op0=ALU.add, op1=ALU.subtract
+        )
+        half_sign(1)
+        nc.vector.tensor_tensor(out=s["e"][:], in0=s["z"][:], in1=s["tz"][:], op=ALU.subtract)
+        half_sign(2)
+        nc.vector.tensor_tensor(out=s["me"][:], in0=s["m"][:], in1=s["e"][:], op=ALU.add)
+        half_sign(3)
+        sc = s["sc"]
+        nc.vector.scalar_tensor_tensor(
+            out=sc[:], in0=s["ln"][:], scalar=1e-6, in1=s["me"][:], op0=ALU.add, op1=ALU.add
+        )
+
+        def w_tile(t):
+            scale_w(t)
+            planes_w(t)
+
+        transpose_x(0, True)
+        evac_x(0, "s")
+        for t in range(4):
+            w_tile(t)
+            evac_w(t, "s")
+        transpose_x(1, True)
+        evac_x(1, "s")
         quant_w(0)
+        half_sign(4)
         quant_w(1)
+        w_tile(4)
+        transpose_x(2, True)
+        half_sign(5)
+        quant_x0(0)
+        evac_w(4, "s")
+        evac_x(2, "s")
         quant_w(2)
         quant_w(3)
-        evac_w(7, "v")
-        new_ost(0)
-        new_ost(2)
-        for i in range(CH):
-            passes(i, 0, "s")
+        passes(0, 0)
+        half_sign(6)
+        w_tile(5)
+        transpose_x(3, True)
+        quant_x0(1)
+        evac_o(0, 0, "s")
+        w_tile(6)
+        passes(1, 0)
+        evac_w(5, "s")
+        half_sign(7)
+        quant_x0(2)
+        w_tile(7)
+        passes(2, 0)
+        evac_w(6, "s")
+        evac_o(1, 0, "s")
+        evac_w(7, "s")
         quant_w(4)
+        evac_x(3, "s")
         quant_w(5)
         quant_w(6)
+        presort(4)
+        presort(5)
         quant_w(7)
+        evac_o(2, 0, "s")
+        transpose_x(4, False)
+        transpose_x(5, False)
+        quant_x0(3)
+        passes(0, 1)
+        passes(1, 1)
+        passes(2, 1)
+        passes(3, 0)
+        passes(3, 1)
+        evac_x(4, "v")
+        evac_o(0, 1, "s")
+        evac_x(5, "v")
+        evac_o(1, 1, "s")
+        store_pair(1)
+        presort(6)
+        presort(7)
+        evac_o(2, 1, "s")
+        quant_x1(4)
+        quant_x1(5)
+        transpose_x(6, False)
+        transpose_x(7, False)
+        evac_o(3, 0, "s")
+        evac_o(3, 1, "s")
+        store_pair(3)
         for i in range(CH):
-            passes(i, 1, "s")
-            if i % 2 == 1:
-                store_pair(i)
-        quant_x(1)
+            presort(2 * CH + i)
+        for t in (4, 5):
+            for h in range(2):
+                passes(t, h)
+                evac_o(t, h, "s")
+        store_pair(5)
+        evac_x(6, "v")
+        evac_x(7, "v")
+        quant_x1(6)
+        quant_x1(7)
+        for i in range(CH):
+            transpose_x(2 * CH + i, False)
+            evac_x(2 * CH + i, "v")
+        for i in range(CH):
+            presort(3 * CH + i)
+        for t in (6, 7):
+            for h in range(2):
+                passes(t, h)
+                evac_o(t, h, "s")
+        store_pair(7)
+        quant_x(2)
 
-        for i in range(CH):
-            presort(2 * CH + i, "v")
-        for c in range(1, NCH):
+        for c in range(2, NCH):
             if c + 1 < NCH:
                 for i in range(CH):
-                    transpose_x(CH * (c + 1) + i)
+                    transpose_x(CH * (c + 1) + i, False)
                 for i in range(CH):
                     evac_x(CH * (c + 1) + i, "v")
             if c + 2 < NCH:
                 for i in range(CH):
-                    presort(CH * (c + 2) + i, "v")
+                    presort(CH * (c + 2) + i)
             if c + 1 < NCH:
                 quant_x(c + 1)
             if c < NCH - 1:
                 for i in range(CH):
                     t = CH * c + i
-                    if i % 2 == 0:
-                        new_ost(t)
-                    passes(t, 0, "s")
-                    passes(t, 1, "s")
-                    if i % 2 == 1:
+                    for h in range(2):
+                        passes(t, h)
+                        evac_o(t, h, "s")
+                    if c >= NCH - 3:
+                        store_one(t)
+                    elif i % 2 == 1:
                         store_pair(t)
         for i in range(CH):
             t = CH * (NCH - 1) + i
             if i < CH - 1:
                 whole = const.tile([P, 1, O], F32, name="olast%d" % i)
-                passes(t, 0, "s", whole[:, 0, 0:512])
-                passes(t, 1, "v", whole[:, 0, 512:O])
+                for h in range(2):
+                    passes(t, h)
+                    evac_o(t, h, "sv"[h], whole[:, 0, 512 * h : 512 * h + 512])
                 nc.sync.dma_start(out=ov[:, t : t + 1, :], in_=whole[:])
             else:
                 for h in range(2):
                     part = const.tile([P, 1, 512], F32, name="opart%d" % h)
-                    passes(t, h, "sv"[h], part[:, 0, :])
+                    passes(t, h)
+                    evac_o(t, h, "sv"[h], part[:, 0, :])
                     nc.sync.dma_start(out=ov[:, t : t + 1, 512 * h : 512 * h + 512], in_=part[:])

@@ -31,10 +31,11 @@ def tile_groupedstelinear_t_kernel(tc, x, weight_logits, raw_scales, out):
 
     with ExitStack() as ctx:
         const = ctx.enter_context(tc.tile_pool(name="const", bufs=1))
+        wrp = ctx.enter_context(tc.tile_pool(name="wrp", bufs=NOT))
         xsp = ctx.enter_context(tc.tile_pool(name="xsp", bufs=8))
         xgp = ctx.enter_context(tc.tile_pool(name="xgp", bufs=2))
         xcp = ctx.enter_context(tc.tile_pool(name="xcp", bufs=3))
-        osp = ctx.enter_context(tc.tile_pool(name="osp", bufs=4))
+        osp = ctx.enter_context(tc.tile_pool(name="osp", bufs=8))
         psum = ctx.enter_context(tc.psum_pool(name="psum", bufs=8))
         ctx.enter_context(tc.manual_schedule())
 
@@ -50,7 +51,7 @@ def tile_groupedstelinear_t_kernel(tc, x, weight_logits, raw_scales, out):
                 xraw[first + i] = tl[:, i, :]
 
         def load_w(t):
-            tl = const.tile([P, K], BF16, name="wraw%d" % t)
+            tl = wrp.tile([P, K], BF16, name="wraw", tag="w", align_bytes=64)
             nc.sync.dma_start(out=tl[:], in_=wv[:, t, :])
             wraw[t] = tl
 
@@ -164,7 +165,7 @@ def tile_groupedstelinear_t_kernel(tc, x, weight_logits, raw_scales, out):
                     op1=ALU.mult,
                 )
 
-        wgrp = [const.tile([P, 2, 512], BF16, name="wgrp%d" % t, align_bytes=64) for t in range(NOT)]
+        wgrp = {}
         wcod = [const.tile([P, 2, 512], U32, name="wcod%d" % h, align_bytes=64) for h in range(2)]
         wpla = [const.tile([P, 2, 512], U8, name="wpla%d" % h, align_bytes=64) for h in range(2)]
         wt = {}
@@ -176,6 +177,7 @@ def tile_groupedstelinear_t_kernel(tc, x, weight_logits, raw_scales, out):
                 nc.tensor.transpose(wt[t][:, j, :], words[:, P * j : P * (j + 1)], ident_f[:])
 
         def evac_w(t, eng):
+            wgrp[t] = wrp.tile([P, 2, 512], BF16, name="wgrp", tag="w", align_bytes=64)
             dst = wgrp[t][:].rearrange("p g c -> p (g c)").bitcast(F32).rearrange(
                 "p (g o u) -> p g o u", g=2, u=2
             )
@@ -366,14 +368,15 @@ def tile_groupedstelinear_t_kernel(tc, x, weight_logits, raw_scales, out):
         for i in range(CH):
             t = CH * (NCH - 1) + i
             if i < CH - 1:
-                whole = const.tile([P, 1, O], F32, name="olast%d" % i)
                 for h in range(2):
                     passes(t, h)
-                    evac_o(t, h, "sv"[h], whole[:, 0, 512 * h : 512 * h + 512])
-                nc.sync.dma_start(out=ov[:, t : t + 1, :], in_=whole[:])
+                    evac_o(t, h, "sv"[h])
+                store_one(t)
             else:
                 for h in range(2):
-                    part = const.tile([P, 1, 512], F32, name="opart%d" % h)
                     passes(t, h)
-                    evac_o(t, h, "sv"[h], part[:, 0, :])
-                    nc.sync.dma_start(out=ov[:, t : t + 1, 512 * h : 512 * h + 512], in_=part[:])
+                    evac_o(t, h, "sv"[h])
+                    part = slice(512 * h, 512 * h + 512)
+                    nc.sync.dma_start(
+                        out=ov[:, t : t + 1, part], in_=ost[t // 2][:, t % 2 : t % 2 + 1, part]
+                    )

@@ -33,9 +33,9 @@ def tile_groupedstelinear_t_kernel(tc, x, weight_logits, raw_scales, out):
         const = ctx.enter_context(tc.tile_pool(name="const", bufs=1))
         wrp = ctx.enter_context(tc.tile_pool(name="wrp", bufs=NOT))
         xsp = ctx.enter_context(tc.tile_pool(name="xsp", bufs=8))
-        xgp = ctx.enter_context(tc.tile_pool(name="xgp", bufs=2))
-        xcp = ctx.enter_context(tc.tile_pool(name="xcp", bufs=3))
-        osp = ctx.enter_context(tc.tile_pool(name="osp", bufs=8))
+        xgp = ctx.enter_context(tc.tile_pool(name="xgp", bufs=3))
+        xcp = ctx.enter_context(tc.tile_pool(name="xcp", bufs=5))
+        osp = ctx.enter_context(tc.tile_pool(name="osp", bufs=6))
         psum = ctx.enter_context(tc.psum_pool(name="psum", bufs=8))
         ctx.enter_context(tc.manual_schedule())
 
@@ -321,62 +321,69 @@ def tile_groupedstelinear_t_kernel(tc, x, weight_logits, raw_scales, out):
         evac_o(3, 0, "s")
         evac_o(3, 1, "s")
         store_pair(3)
-        for i in range(CH):
-            presort(2 * CH + i)
-        for t in (4, 5):
+        def presort_chunk(c):
+            for i in range(CH):
+                presort(CH * c + i)
+
+        def transpose_chunk(c):
+            for i in range(CH):
+                transpose_x(CH * c + i, False)
+
+        def evac_chunk(c, from_s):
+            for i in range(CH):
+                evac_x(CH * c + i, "s" if i < from_s else "v")
+
+        def multiply(t, engines):
             for h in range(2):
                 passes(t, h)
-                evac_o(t, h, "s")
+                evac_o(t, h, engines[h])
+
+        presort_chunk(2)
+        for t in (4, 5):
+            multiply(t, "ss")
         store_pair(5)
         evac_x(6, "v")
         evac_x(7, "v")
         quant_x1(6)
         quant_x1(7)
-        for i in range(CH):
-            transpose_x(2 * CH + i, False)
-            evac_x(2 * CH + i, "v")
-        for i in range(CH):
-            presort(3 * CH + i)
-        for t in (6, 7):
-            for h in range(2):
-                passes(t, h)
-                evac_o(t, h, "s")
-        store_pair(7)
+        presort_chunk(3)
+        transpose_chunk(2)
+        evac_chunk(2, 1)
+        transpose_chunk(3)
+        evac_x(12, "s")
+        evac_x(13, "v")
         quant_x(2)
+        evac_x(14, "v")
+        evac_x(15, "v")
+        for t in (6, 7):
+            multiply(t, "ss")
+        store_pair(7)
+        presort_chunk(4)
+        quant_x(3)
+        presort_chunk(5)
 
         for c in range(2, NCH):
-            if c + 1 < NCH:
-                for i in range(CH):
-                    transpose_x(CH * (c + 1) + i, False)
-                for i in range(CH):
-                    evac_x(CH * (c + 1) + i, "v")
-            if c + 2 < NCH:
-                for i in range(CH):
-                    presort(CH * (c + 2) + i)
-            if c + 1 < NCH:
+            if c % 2 == 1 and c + 2 < NCH:
+                transpose_chunk(c + 1)
+                evac_chunk(c + 1, 0)
+                transpose_chunk(c + 2)
+                evac_chunk(c + 2, 0)
                 quant_x(c + 1)
-            if c < NCH - 1:
-                for i in range(CH):
-                    t = CH * c + i
+                if c + 4 < NCH:
+                    presort_chunk(c + 3)
+                    presort_chunk(c + 4)
+                quant_x(c + 2)
+            for i in range(CH):
+                t = CH * c + i
+                multiply(t, "ss" if c + 2 < NCH else "sv")
+                if t == NT - 1:
                     for h in range(2):
-                        passes(t, h)
-                        evac_o(t, h, "s")
-                    if c >= NCH - 3:
-                        store_one(t)
-                    elif i % 2 == 1:
-                        store_pair(t)
-        for i in range(CH):
-            t = CH * (NCH - 1) + i
-            if i < CH - 1:
-                for h in range(2):
-                    passes(t, h)
-                    evac_o(t, h, "sv"[h])
-                store_one(t)
-            else:
-                for h in range(2):
-                    passes(t, h)
-                    evac_o(t, h, "sv"[h])
-                    part = slice(512 * h, 512 * h + 512)
-                    nc.sync.dma_start(
-                        out=ov[:, t : t + 1, part], in_=ost[t // 2][:, t % 2 : t % 2 + 1, part]
-                    )
+                        part = slice(512 * h, 512 * h + 512)
+                        nc.sync.dma_start(
+                            out=ov[:, t : t + 1, part],
+                            in_=ost[t // 2][:, t % 2 : t % 2 + 1, part],
+                        )
+                elif c >= NCH - 3:
+                    store_one(t)
+                elif i % 2 == 1:
+                    store_pair(t)

@@ -322,16 +322,16 @@ def tile_groupedstelinear_t_kernel(tc, x, weight_logits, raw_scales, out):
         evac_o(3, 1, "s")
         store_pair(3)
         def presort_chunk(c):
-            for i in range(CH):
+            for i in range(1, CH):
                 presort(CH * c + i)
 
         def transpose_chunk(c):
             for i in range(CH):
-                transpose_x(CH * c + i, False)
+                transpose_x(CH * c + i, i == 0)
 
-        def evac_chunk(c, from_s):
+        def evac_chunk(c):
             for i in range(CH):
-                evac_x(CH * c + i, "s" if i < from_s else "v")
+                evac_x(CH * c + i, "v" if i else "s")
 
         def multiply(t, engines):
             for h in range(2):
@@ -348,7 +348,7 @@ def tile_groupedstelinear_t_kernel(tc, x, weight_logits, raw_scales, out):
         quant_x1(7)
         presort_chunk(3)
         transpose_chunk(2)
-        evac_chunk(2, 1)
+        evac_chunk(2)
         transpose_chunk(3)
         evac_x(12, "s")
         evac_x(13, "v")
@@ -365,9 +365,9 @@ def tile_groupedstelinear_t_kernel(tc, x, weight_logits, raw_scales, out):
         for c in range(2, NCH):
             if c % 2 == 1 and c + 2 < NCH:
                 transpose_chunk(c + 1)
-                evac_chunk(c + 1, 0)
+                evac_chunk(c + 1)
                 transpose_chunk(c + 2)
-                evac_chunk(c + 2, 0)
+                evac_chunk(c + 2)
                 quant_x(c + 1)
                 if c + 4 < NCH:
                     presort_chunk(c + 3)

@@ -26,12 +26,12 @@ def tile_groupedstelinear_t_kernel(tc, x, weight_logits, raw_scales, out):
     nc = tc.nc
     xv = x.flatten_outer_dims().rearrange("(p t) k -> p t k", t=NT)
     ov = out.flatten_outer_dims().rearrange("(p t) o -> p t o", t=NT)
-    wv = weight_logits.rearrange("(t p) i -> p t i", p=P)
-    sv = raw_scales.rearrange("(t p) g -> p t g", p=P)
+    wv = weight_logits.rearrange("(h p j) i -> p h j i", h=2, j=4)
+    sv = raw_scales.rearrange("(h p j) g -> p h (j g)", h=2, j=4)
 
     with ExitStack() as ctx:
         const = ctx.enter_context(tc.tile_pool(name="const", bufs=1))
-        wrp = ctx.enter_context(tc.tile_pool(name="wrp", bufs=NOT))
+        wrp = ctx.enter_context(tc.tile_pool(name="wrp", bufs=NOT // 2))
         xsp = ctx.enter_context(tc.tile_pool(name="xsp", bufs=8))
         xgp = ctx.enter_context(tc.tile_pool(name="xgp", bufs=3))
         xcp = ctx.enter_context(tc.tile_pool(name="xcp", bufs=5))
@@ -39,10 +39,11 @@ def tile_groupedstelinear_t_kernel(tc, x, weight_logits, raw_scales, out):
         psum = ctx.enter_context(tc.psum_pool(name="psum", bufs=8))
         ctx.enter_context(tc.manual_schedule())
 
-        sraw = const.tile([P, NOT, 8], BF16, name="sraw")
+        sraw = const.tile([P, 2, 32], BF16, name="sraw")
         nc.sync.dma_start(out=sraw[:], in_=sv)
         xraw = {}
         wraw = {}
+        wload = {}
 
         def load_x(first, count):
             tl = const.tile([P, count, K], BF16, name="xraw%d" % first)
@@ -50,21 +51,30 @@ def tile_groupedstelinear_t_kernel(tc, x, weight_logits, raw_scales, out):
             for i in range(count):
                 xraw[first + i] = tl[:, i, :]
 
-        def load_w(t):
-            tl = wrp.tile([P, K], BF16, name="wraw", tag="w", align_bytes=64)
-            nc.sync.dma_start(out=tl[:], in_=wv[:, t, :])
-            wraw[t] = tl
+        def load_w(first, count):
+            if first % 2 == 0:
+                tl = wrp.tile([P, 2, K], BF16, name="wraw", tag="w", align_bytes=64)
+                for i in range(2):
+                    wraw[first + i] = tl[:, i, :]
+                wload[first // 2] = tl
+            rows = slice(first % 2, first % 2 + count)
+            nc.sync.dma_start(
+                out=wload[first // 2][:, rows, :],
+                in_=wv[:, first // 4, first % 4 : first % 4 + count, :],
+            )
 
         for t in range(4):
-            load_w(t)
+            load_w(t, 1)
         for i in range(4):
             load_x(i, 1)
-        for t in range(4, NOT):
-            load_w(t)
-        load_x(4, 2)
-        load_x(6, 2)
-        for c in range(2, NCH):
-            load_x(CH * c, CH)
+        load_w(4, 1)
+        load_w(5, 1)
+        load_w(6, 2)
+        load_x(4, 4)
+        load_x(8, 4)
+        load_x(12, 4)
+        load_x(16, 8)
+        load_x(24, 8)
 
         ident_f = const.tile([P, P], F32, name="ident_f")
         make_identity(nc, ident_f[:])
@@ -177,8 +187,11 @@ def tile_groupedstelinear_t_kernel(tc, x, weight_logits, raw_scales, out):
                 nc.tensor.transpose(wt[t][:, j, :], words[:, P * j : P * (j + 1)], ident_f[:])
 
         def evac_w(t, eng):
-            wgrp[t] = wrp.tile([P, 2, 512], BF16, name="wgrp", tag="w", align_bytes=64)
-            dst = wgrp[t][:].rearrange("p g c -> p (g c)").bitcast(F32).rearrange(
+            if t % 2 == 0:
+                pair = wrp.tile([P, 2, 2, 512], BF16, name="wgrp", tag="w", align_bytes=64)
+                for i in range(2):
+                    wgrp[t + i] = pair[:, i]
+            dst = wgrp[t].rearrange("p g c -> p (g c)").bitcast(F32).rearrange(
                 "p (g o u) -> p g o u", g=2, u=2
             )
             src = wt[t][:].rearrange("p (g u) o -> p g o u", u=2)
@@ -220,10 +233,12 @@ def tile_groupedstelinear_t_kernel(tc, x, weight_logits, raw_scales, out):
                 if t // 2 not in ost:
                     ost[t // 2] = osp.tile([P, 2, O], F32, name="ost", tag="ost")
                 dst = ost[t // 2][:, t % 2, 512 * h : 512 * h + 512]
+            dst = dst.rearrange("p (q j) -> p q j", j=4)
+            src = acc[t, h][:].rearrange("p (j q) -> p q j", j=4)
             if eng == "s":
-                nc.scalar.copy(out=dst, in_=acc[t, h][:])
+                nc.scalar.copy(out=dst, in_=src)
             else:
-                nc.vector.tensor_copy(out=dst, in_=acc[t, h][:])
+                nc.vector.tensor_copy(out=dst, in_=src)
 
         def store_pair(t):
             nc.sync.dma_start(out=ov[:, t - 1 : t + 1, :], in_=ost[t // 2][:])
@@ -231,7 +246,7 @@ def tile_groupedstelinear_t_kernel(tc, x, weight_logits, raw_scales, out):
         def store_one(t):
             nc.sync.dma_start(out=ov[:, t : t + 1, :], in_=ost[t // 2][:, t % 2 : t % 2 + 1, :])
 
-        v = sraw[:].rearrange("p t g -> p (t g)")
+        v = sraw[:].rearrange("p h c -> p (h c)")
         names = ("av", "z", "ln", "m", "tz", "e", "me", "sc")
         s = {n: const.tile([P, 64], F32, name=n) for n in names}
         nc.scalar.activation(out=s["av"][:], in_=v, func=ACT.Abs)
@@ -246,11 +261,11 @@ def tile_groupedstelinear_t_kernel(tc, x, weight_logits, raw_scales, out):
         nc.vector.tensor_tensor(out=s["e"][:], in0=s["z"][:], in1=s["tz"][:], op=ALU.subtract)
         half_sign(2)
         nc.vector.tensor_tensor(out=s["me"][:], in0=s["m"][:], in1=s["e"][:], op=ALU.add)
-        half_sign(3)
         sc = s["sc"]
         nc.vector.scalar_tensor_tensor(
             out=sc[:], in0=s["ln"][:], scalar=1e-6, in1=s["me"][:], op0=ALU.add, op1=ALU.add
         )
+        half_sign(3)
 
         def w_tile(t):
             scale_w(t)

from contextlib import ExitStack

import concourse.mybir as mybir
from concourse.masks import make_identity

FLOPS = 2 * 4096 * 1024 * 1024

BF16 = mybir.dt.bfloat16
F32 = mybir.dt.float32
U32 = mybir.dt.uint32
U8 = mybir.dt.uint8
FP8X4 = mybir.dt.float8_e4m3fn_x4
ALU = mybir.AluOpType
ACT = mybir.ActivationFunctionType

P = 128
K = 1024
O = 1024
NT = 32
CH = 4
NCH = NT // CH
NOT = O // P


def tile_groupedstelinear_t_kernel(tc, x, weight_logits, raw_scales, out):
    nc = tc.nc
    xv = x.flatten_outer_dims().rearrange("(p t) k -> p t k", t=NT)
    ov = out.flatten_outer_dims().rearrange("(p t) o -> p t o", t=NT)
    wv = weight_logits.rearrange("(h p j) i -> p h j i", h=2, j=4)
    sv = raw_scales.rearrange("(h p j) g -> p h (j g)", h=2, j=4)

    with ExitStack() as ctx:
        const = ctx.enter_context(tc.tile_pool(name="const", bufs=1))
        wrp = ctx.enter_context(tc.tile_pool(name="wrp", bufs=NOT // 2))
        xsp = ctx.enter_context(tc.tile_pool(name="xsp", bufs=8))
        xgp = ctx.enter_context(tc.tile_pool(name="xgp", bufs=3))
        xcp = ctx.enter_context(tc.tile_pool(name="xcp", bufs=5))
        osp = ctx.enter_context(tc.tile_pool(name="osp", bufs=6))
        psum = ctx.enter_context(tc.psum_pool(name="psum", bufs=8))
        ctx.enter_context(tc.manual_schedule())

        sraw = const.tile([P, 2, 32], BF16, name="sraw")
        nc.sync.dma_start(out=sraw[:], in_=sv)
        xraw = {}
        wraw = {}
        wload = {}

        def load_x(first, count):
            tl = const.tile([P, count, K], BF16, name="xraw%d" % first)
            nc.sync.dma_start(out=tl[:], in_=xv[:, first : first + count, :])
            for i in range(count):
                xraw[first + i] = tl[:, i, :]

        def load_w(first, count):
            if first % 2 == 0:
                tl = wrp.tile([P, 2, K], BF16, name="wraw", tag="w", align_bytes=64)
                for i in range(2):
                    wraw[first + i] = tl[:, i, :]
                wload[first // 2] = tl
            rows = slice(first % 2, first % 2 + count)
            nc.sync.dma_start(
                out=wload[first // 2][:, rows, :],
                in_=wv[:, first // 4, first % 4 : first % 4 + count, :],
            )

        for t in range(4):
            load_w(t, 1)
        for i in range(4):
            load_x(i, 1)
        load_w(4, 1)
        load_w(5, 1)
        load_w(6, 2)
        load_x(4, 4)
        load_x(8, 4)
        load_x(12, 4)
        load_x(16, 8)
        load_x(24, 8)

        ident_f = const.tile([P, P], F32, name="ident_f")
        make_identity(nc, ident_f[:])

        xs = {}
        xt = {}
        xg = {}
        xc = {}
        xp = {}

        def presort(t):
            xs[t] = xsp.tile([P, K], BF16, name="xs", tag="xs")
            nc.vector.tensor_copy(
                out=xs[t][:].bitcast(F32).rearrange("p (g u q) -> p g u q", g=2, u=2),
                in_=xraw[t].bitcast(F32).rearrange("p (g q u) -> p g u q", g=2, u=2),
            )

        def transpose_x(t, direct):
            xt[t] = psum.tile([P, 4, P], F32, name="xt", tag="bank")
            words = (xraw[t] if direct else xs[t][:]).bitcast(F32)
            for j in range(4):
                g, u = divmod(j, 2)
                if direct:
                    cols = words[:, 256 * g + u : 256 * (g + 1) : 2]
                else:
                    cols = words[:, P * j : P * (j + 1)]
                nc.tensor.transpose(xt[t][:, j, :], cols, ident_f[:])

        def evac_x(t, eng):
            c, i = divmod(t, CH)
            if c == 0:
                xg[t] = const.tile([P, K], BF16, name="xg0_%d" % i, align_bytes=64)
                grouped = xg[t][:]
            else:
                if -c not in xg:
                    xg[-c] = xgp.tile([P, CH, K], BF16, name="xg", tag="xg", align_bytes=64)
                grouped = xg[-c][:, i, :]
            dst = grouped.bitcast(F32).rearrange("p (g o u) -> p g o u", g=2, u=2)
            src = xt[t][:].rearrange("p (g u) o -> p g o u", u=2)
            if eng == "s":
                nc.scalar.copy(out=dst, in_=src)
            else:
                nc.vector.tensor_copy(out=dst, in_=src)

        def codes_x(c):
            xc[c] = xcp.tile([P, CH * 256], U32, name="xc", tag="xc", align_bytes=64)
            xp[c] = xcp.tile([P, CH * 256], U8, name="xp", tag="xp", align_bytes=64)

        def quant_x0(i):
            if i == 0:
                codes_x(0)
            nc.vector.quantize_mx(
                out=xc[0][:, 256 * i : 256 * (i + 1)].bitcast(FP8X4),
                scales=xp[0][:, 256 * i : 256 * (i + 1)],
                in_=xg[i][:],
            )

        def quant_x1(t):
            c, i = divmod(t, CH)
            if i == 0:
                codes_x(c)
            nc.vector.quantize_mx(
                out=xc[c][:, 256 * i : 256 * (i + 1)].bitcast(FP8X4),
                scales=xp[c][:, 256 * i : 256 * (i + 1)],
                in_=xg[-c][:, i, :],
            )

        def quant_x(c):
            codes_x(c)
            nc.vector.quantize_mx(
                out=xc[c][:].bitcast(FP8X4),
                scales=xp[c][:],
                in_=xg[-c][:].rearrange("p i k -> p (i k)"),
            )

        hs = {}

        def half_sign(t):
            hs[t] = const.tile([P, K], BF16, name="hs%d" % t)
            for g in range(2):
                nc.vector.tensor_scalar(
                    out=hs[t][:, 512 * g : 512 * g + 512].rearrange("p (u q e) -> p u q e", u=2, e=2),
                    in0=wraw[t][:, 512 * g : 512 * g + 512].rearrange("p (q u e) -> p u q e", u=2, e=2),
                    scalar1=0.0, scalar2=0.5,
                    op0=ALU.is_ge, op1=ALU.subtract,
                )

        def scale_w(t):
            v = hs[t][:].rearrange("p (g u a r) -> p g u a r", g=2, u=2, a=4)
            for grp in range(8):
                g, a = divmod(grp, 4)
                nc.vector.tensor_scalar(
                    out=v[:, g, :, a, :],
                    in0=v[:, g, :, a, :],
                    scalar1=2.0,
                    scalar2=sc[:, t * 8 + grp : t * 8 + grp + 1],
                    op0=ALU.mult,
                    op1=ALU.mult,
                )

        wgrp = {}
        wcod = [const.tile([P, 2, 512], U32, name="wcod%d" % h, align_bytes=64) for h in range(2)]
        wpla = [const.tile([P, 2, 512], U8, name="wpla%d" % h, align_bytes=64) for h in range(2)]
        wt = {}

        def planes_w(t):
            wt[t] = psum.tile([P, 4, P], F32, name="wt", tag="bank")
            words = hs[t][:].bitcast(F32)
            for j in range(4):
                nc.tensor.transpose(wt[t][:, j, :], words[:, P * j : P * (j + 1)], ident_f[:])

        def evac_w(t, eng):
            if t % 2 == 0:
                pair = wrp.tile([P, 2, 2, 512], BF16, name="wgrp", tag="w", align_bytes=64)
                for i in range(2):
                    wgrp[t + i] = pair[:, i]
            dst = wgrp[t].rearrange("p g c -> p (g c)").bitcast(F32).rearrange(
                "p (g o u) -> p g o u", g=2, u=2
            )
            src = wt[t][:].rearrange("p (g u) o -> p g o u", u=2)
            if eng == "s":
                nc.scalar.copy(out=dst, in_=src)
            else:
                nc.vector.tensor_copy(out=dst, in_=src)

        def quant_w(t):
            h, j = divmod(t, 4)
            for g in range(2):
                nc.vector.quantize_mx(
                    out=wcod[h][:, g, P * j : P * (j + 1)].bitcast(FP8X4),
                    scales=wpla[h][:, g, P * j : P * (j + 1)],
                    in_=wgrp[t][:, g, :],
                )

        ost = {}

        acc = {}

        def passes(t, h):
            c, i = divmod(t, CH)
            acc[t, h] = psum.tile([P, 512], F32, name="acc", tag="bank")
            for g in range(2):
                col = (2 * i + g) * P
                nc.tensor.matmul_mx(
                    out=acc[t, h][:],
                    lhsT=xc[c][:, col : col + P].bitcast(FP8X4),
                    lhsT_scale=xp[c][:, col : col + P],
                    rhs=wcod[h][:, g, :].bitcast(FP8X4),
                    rhs_scale=wpla[h][:, g, :],
                    start=(g == 0),
                    stop=(g == 1),
                )

        def evac_o(t, h, eng, dst=None):
            if dst is None:
                if t // 2 not in ost:
                    ost[t // 2] = osp.tile([P, 2, O], F32, name="ost", tag="ost")
                dst = ost[t // 2][:, t % 2, 512 * h : 512 * h + 512]
            dst = dst.rearrange("p (q j) -> p q j", j=4)
            src = acc[t, h][:].rearrange("p (j q) -> p q j", j=4)
            if eng == "s":
                nc.scalar.copy(out=dst, in_=src)
            else:
                nc.vector.tensor_copy(out=dst, in_=src)

        def store_pair(t):
            nc.sync.dma_start(out=ov[:, t - 1 : t + 1, :], in_=ost[t // 2][:])

        def store_one(t):
            nc.sync.dma_start(out=ov[:, t : t + 1, :], in_=ost[t // 2][:, t % 2 : t % 2 + 1, :])

        v = sraw[:].rearrange("p h c -> p (h c)")
        names = ("av", "z", "ln", "m", "tz", "e", "me", "sc")
        s = {n: const.tile([P, 64], F32, name=n) for n in names}
        nc.scalar.activation(out=s["av"][:], in_=v, func=ACT.Abs)
        nc.scalar.activation(out=s["z"][:], in_=s["av"][:], func=ACT.Exp, scale=-1.0)
        nc.scalar.activation(out=s["ln"][:], in_=s["z"][:], func=ACT.Ln, bias=1.0)
        nc.vector.tensor_scalar(out=s["m"][:], in0=v, scalar1=0.0, scalar2=None, op0=ALU.max)
        half_sign(0)
        nc.vector.tensor_scalar(
            out=s["tz"][:], in0=s["z"][:], scalar1=1.0, scalar2=1.0, op0=ALU.add, op1=ALU.subtract
        )
        half_sign(1)
        nc.vector.tensor_tensor(out=s["e"][:], in0=s["z"][:], in1=s["tz"][:], op=ALU.subtract)
        half_sign(2)
        nc.vector.tensor_tensor(out=s["me"][:], in0=s["m"][:], in1=s["e"][:], op=ALU.add)
        sc = s["sc"]
        nc.vector.scalar_tensor_tensor(
            out=sc[:], in0=s["ln"][:], scalar=1e-6, in1=s["me"][:], op0=ALU.add, op1=ALU.add
        )
        half_sign(3)

        def w_tile(t):
            scale_w(t)
            planes_w(t)

        transpose_x(0, True)
        evac_x(0, "s")
        for t in range(4):
            w_tile(t)
            evac_w(t, "s")
        transpose_x(1, True)
        evac_x(1, "s")
        quant_w(0)
        half_sign(4)
        quant_w(1)
        w_tile(4)
        transpose_x(2, True)
        half_sign(5)
        quant_x0(0)
        evac_w(4, "s")
        evac_x(2, "s")
        quant_w(2)
        quant_w(3)
        passes(0, 0)
        half_sign(6)
        w_tile(5)
        transpose_x(3, True)
        quant_x0(1)
        evac_o(0, 0, "s")
        w_tile(6)
        passes(1, 0)
        evac_w(5, "s")
        half_sign(7)
        quant_x0(2)
        w_tile(7)
        passes(2, 0)
        evac_w(6, "s")
        evac_o(1, 0, "s")
        evac_w(7, "s")
        quant_w(4)
        evac_x(3, "s")
        quant_w(5)
        quant_w(6)
        presort(4)
        presort(5)
        quant_w(7)
        evac_o(2, 0, "s")
        transpose_x(4, False)
        transpose_x(5, False)
        quant_x0(3)
        passes(0, 1)
        passes(1, 1)
        passes(2, 1)
        passes(3, 0)
        passes(3, 1)
        evac_x(4, "v")
        evac_o(0, 1, "s")
        evac_x(5, "v")
        evac_o(1, 1, "s")
        store_pair(1)
        presort(6)
        presort(7)
        evac_o(2, 1, "s")
        quant_x1(4)
        quant_x1(5)
        transpose_x(6, False)
        transpose_x(7, False)
        evac_o(3, 0, "s")
        evac_o(3, 1, "s")
        store_pair(3)
        def presort_chunk(c):
            for i in range(1, CH):
                presort(CH * c + i)

        def transpose_chunk(c):
            for i in range(CH):
                transpose_x(CH * c + i, i == 0)

        def evac_chunk(c):
            for i in range(CH):
                evac_x(CH * c + i, "v" if i else "s")

        def multiply(t, engines):
            for h in range(2):
                passes(t, h)
                evac_o(t, h, engines[h])

        presort_chunk(2)
        for t in (4, 5):
            multiply(t, "ss")
        store_pair(5)
        evac_x(6, "v")
        evac_x(7, "v")
        quant_x1(6)
        quant_x1(7)
        presort_chunk(3)
        transpose_chunk(2)
        evac_chunk(2)
        transpose_chunk(3)
        evac_x(12, "s")
        evac_x(13, "v")
        quant_x(2)
        evac_x(14, "v")
        evac_x(15, "v")
        for t in (6, 7):
            multiply(t, "ss")
        store_pair(7)
        presort_chunk(4)
        quant_x(3)
        presort_chunk(5)

        for c in range(2, NCH):
            if c % 2 == 1 and c + 2 < NCH:
                transpose_chunk(c + 1)
                evac_chunk(c + 1)
                transpose_chunk(c + 2)
                evac_chunk(c + 2)
                quant_x(c + 1)
                if c + 4 < NCH:
                    presort_chunk(c + 3)
                    presort_chunk(c + 4)
                quant_x(c + 2)
            for i in range(CH):
                t = CH * c + i
                multiply(t, "ss" if c + 2 < NCH else "sv")
                if t == NT - 1:
                    for h in range(2):
                        part = slice(512 * h, 512 * h + 512)
                        nc.sync.dma_start(
                            out=ov[:, t : t + 1, part],
                            in_=ost[t // 2][:, t % 2 : t % 2 + 1, part],
                        )
                elif c >= NCH - 3:
                    store_one(t)
                elif i % 2 == 1:
                    store_pair(t)
